import numpy as np
import ml_dtypes


def mxq(x, axis, fmt="e4m3"):
    dtype, down = {"e4m3": (ml_dtypes.float8_e4m3fn, 7), "e5m2": (ml_dtypes.float8_e5m2, 14)}[fmt]
    v = np.moveaxis(np.asarray(x, np.float32).astype(ml_dtypes.bfloat16).astype(np.float64), axis, -1)
    blocks = v.reshape(v.shape[:-1] + (-1, 32))
    amax = np.abs(blocks).max(-1, keepdims=True)
    byte = np.maximum(np.where(amax > 0, np.frexp(amax)[1] - 1 + 127, 0) - down, 1)
    scale = np.exp2(byte - 127.0)
    codes = (blocks / scale).astype(np.float32).astype(dtype).astype(np.float64)
    return np.moveaxis((codes * scale).reshape(v.shape), -1, axis)


WIDE = False


def mx_kscale(k):
    if not WIDE:
        return np.ones(k)
    levels = np.array([10, -10, 5, -5, 0])
    a = np.random.permutation(np.resize(levels, k // 512 * 4)).reshape(k // 512, 4)
    idx = np.arange(k)
    return np.exp2(a[idx // 512, idx % 128 // 32])


BF16 = ml_dtypes.bfloat16


def bf(x):
    return np.asarray(x, np.float32).astype(BF16)


def f64(x):
    return np.asarray(x).astype(np.float64)


B, S, D = 128, 16, 512
EPS = 1e-9


def layernorm(x, gain, bias_):
    mu = x.mean(-1, keepdims=True)
    sd = x.std(-1, keepdims=True)
    return gain * (x - mu) / (sd + EPS) + bias_


def setup_inputs():
    s, t = mx_kscale(D), mx_kscale(D)
    return {
        "c_att": bf(np.random.standard_normal((B, S, D)) * 0.4 * s),
        "mlp_kernel_1": bf(np.random.standard_normal((D, D)) / np.sqrt(D) / s[:, None]),
        "mlp_kernel_2": bf(np.random.standard_normal((D, D)) / np.sqrt(D) / t[:, None]),
        "mlp_gain_1": bf((1.0 + 0.1 * np.random.standard_normal(D)) * t),
        "mlp_gain_2": bf(1.0 + 0.1 * np.random.standard_normal(D)),
        "mlp_bias_1": bf(0.1 * np.random.standard_normal(D) * t),
        "mlp_bias_2": bf(0.1 * np.random.standard_normal(D)),
    }


def reference(c_att, mlp_kernel_1, mlp_kernel_2, mlp_gain_1, mlp_gain_2, mlp_bias_1, mlp_bias_2):
    y1 = mxq(f64(c_att), 2, "e4m3") @ mxq(f64(mlp_kernel_1), 0, "e4m3")
    h = np.maximum(layernorm(y1, f64(mlp_gain_1), f64(mlp_bias_1)), 0.0)
    y2 = mxq(h, 2, "e4m3") @ mxq(f64(mlp_kernel_2), 0, "e4m3")
    return layernorm(y2, f64(mlp_gain_2), f64(mlp_bias_2))

@@ -1,0 +1,229 @@
+from contextlib import ExitStack
+
+import concourse.mybir as mybir
+from concourse.masks import make_identity
+
+F32 = mybir.dt.float32
+BF16 = mybir.dt.bfloat16
+U32 = mybir.dt.uint32
+U8 = mybir.dt.uint8
+FP8X4 = mybir.dt.float8_e4m3fn_x4
+ACT = mybir.ActivationFunctionType
+ALU = mybir.AluOpType
+
+P = 128
+S = 16
+D = 512
+EPS = 1e-9
+N_PAIRS = S // 2
+FLOPS = 2 * 2 * (P * S) * D * D
+
+V_STATS_PAIRS = (3, 7)
+
+
+def tile_rlstmcell_pa_kernel(
+    tc, c_att, mlp_kernel_1, mlp_kernel_2, mlp_gain_1, mlp_gain_2, mlp_bias_1, mlp_bias_2, out
+):
+    nc = tc.nc
+    with ExitStack() as ctx:
+        const = ctx.enter_context(tc.tile_pool(name="const", bufs=1))
+        work = ctx.enter_context(tc.tile_pool(name="work", bufs=3))
+        small = ctx.enter_context(tc.tile_pool(name="small", bufs=4))
+        psum = ctx.enter_context(tc.psum_pool(name="psum", bufs=1))
+
+        warm_in = const.tile([P, 1], F32)
+        warm_out = const.tile([P, 1], F32)
+        nc.vector.memset(warm_in[:], 1.0)
+        nc.scalar.sqrt(out=warm_out[:], in_=warm_in[:])
+        rows1 = const.tile([P, P], BF16)
+        nc.vector.memset(rows1[:], 0.0)
+        rows2 = const.tile([P, 2 * D], BF16)
+        nc.vector.memset(rows2[:], 0.0)
+        ones = const.tile([P, P], BF16)
+        nc.vector.memset(ones[:], 1.0)
+        ident = const.tile([P, P], F32)
+        make_identity(nc, ident[:])
+
+        nc.scalar.dma_start(out=rows1[0:4, :], in_=mlp_gain_1.rearrange("(j c) -> j c", c=P))
+        nc.scalar.dma_start(out=rows1[4:8, :], in_=mlp_bias_1.rearrange("(j c) -> j c", c=P))
+        nc.scalar.dma_start(out=rows2[0:1, 0:D], in_=mlp_gain_2.rearrange("(o c) -> o c", o=1))
+        nc.scalar.dma_start(out=rows2[0:1, D : 2 * D], in_=mlp_bias_2.rearrange("(o c) -> o c", o=1))
+
+        w1raw = const.tile([P, 4, D], BF16)
+        nc.sync.dma_start(
+            out=w1raw[:].rearrange("q (u e) c -> q u e c", u=2),
+            in_=mlp_kernel_1.rearrange("(u q e) c -> q u e c", u=2, e=2),
+        )
+        x_all = const.tile([P, S, D], BF16)
+        w2raw = const.tile([P, 4, D], BF16)
+        for lo, hi in ((0, 2), (2, 4), (4, 8)):
+            nc.sync.dma_start(out=x_all[:, lo:hi, :], in_=c_att[:, lo:hi, :])
+        nc.sync.dma_start(out=w2raw[:], in_=mlp_kernel_2.rearrange("(j p) c -> p j c", p=P))
+        for lo, hi in ((8, 12), (12, 16)):
+            nc.sync.dma_start(out=x_all[:, lo:hi, :], in_=c_att[:, lo:hi, :])
+        x_words = x_all[:].rearrange("p s d -> p (s d)").bitcast(F32)
+
+        rows1f = const.tile([P, P], F32)
+        nc.vector.tensor_copy(out=rows1f[:], in_=rows1[:])
+        gb1_ps = psum.tile([P, D], F32, tag="xt", bufs=1)
+        nc.tensor.transpose(out=gb1_ps[:, 0:P], in_=rows1f[:], identity=ident[:])
+        gb1 = const.tile([P, 8], F32)
+        nc.vector.tensor_copy(out=gb1[:], in_=gb1_ps[:, 0:8])
+        gb2 = const.tile([P, 2, D], F32)
+        for h in range(2):
+            gb2_ps = psum.tile([P, D], F32, tag="y2", bufs=2)
+            nc.tensor.matmul(out=gb2_ps[:], lhsT=ones[:], rhs=rows2[:, h * D : (h + 1) * D], start=True, stop=True)
+            nc.scalar.copy(out=gb2[:, h, :], in_=gb2_ps[:])
+
+        def quantise_weight(raw, label):
+            grouped = const.tile([P, D, 4], BF16, align_bytes=64, name=label + "_grouped")
+            nc.vector.tensor_copy(
+                out=grouped[:].rearrange("p (c i) t -> p c t i", i=4),
+                in_=raw[:].rearrange("p t (c i) -> p c t i", i=4),
+            )
+            codes = const.tile([P, D], U32, align_bytes=64, name=label + "_codes")
+            scales = const.tile([P, D], U8, align_bytes=64, name=label + "_scales")
+            nc.vector.quantize_mx(
+                out=codes[:].bitcast(FP8X4), scales=scales[:], in_=grouped[:].rearrange("p c t -> p (c t)")
+            )
+            return codes, scales
+
+        w1codes, w1scales = quantise_weight(w1raw, "w1")
+
+        xcodes = const.tile([P, S * P], U32, align_bytes=64)
+        xscales = const.tile([P, S * P], U8, align_bytes=64)
+
+        def stage_x(p):
+            xt = psum.tile([P, D], F32, tag="xt", bufs=1)
+            for i in range(2):
+                for u in range(2):
+                    col = (2 * p + i) * 256 + u * P
+                    nc.tensor.transpose(
+                        out=xt[:, (2 * i + u) * P : (2 * i + u + 1) * P],
+                        in_=x_words[:, col : col + P],
+                        identity=ident[:],
+                    )
+            xg = work.tile([P, 2 * D], BF16, align_bytes=64, tag="xg")
+            nc.scalar.copy(
+                out=xg[:].bitcast(F32).rearrange("p (i k u) -> p i k u", i=2, u=2),
+                in_=xt[:].rearrange("p (i u k) -> p i k u", i=2, u=2),
+            )
+            cols = slice(2 * p * P, (2 * p + 2) * P)
+            nc.vector.quantize_mx(out=xcodes[:, cols].bitcast(FP8X4), scales=xscales[:, cols], in_=xg[:])
+
+        def inverse_deviation(sum_ap, divisor, label):
+            sd = small.tile([P, 1], F32, tag=label + "_sd")
+            nc.scalar.activation(out=sd[:], in_=sum_ap, func=ACT.Sqrt, scale=1.0 / divisor)
+            sde = small.tile([P, 1], F32, tag=label + "_sde")
+            nc.vector.tensor_scalar_add(out=sde[:], in0=sd[:], scalar1=EPS)
+            r = small.tile([P, 1], F32, tag=label + "_r")
+            nc.vector.reciprocal(out=r[:], in_=sde[:])
+            return r
+
+        def vector_stats(y, label):
+            st = small.tile([P, 6], F32, tag=label + "_st")
+            nc.vector.bn_stats(out=st[:], in_=y[:])
+            mv = small.tile([P, 2], F32, tag=label + "_mv")
+            nc.vector.bn_aggr(out=mv[:], in_=st[:])
+            return mv
+
+        def stage_a(p, z):
+            for i in range(2):
+                s = 2 * p + i
+                y1 = psum.tile([P, D], F32, tag="y1", bufs=2)
+                nc.tensor.matmul_mx(
+                    out=y1[:],
+                    lhsT=xcodes[:, s * P : (s + 1) * P].bitcast(FP8X4),
+                    lhsT_scale=xscales[:, s * P : (s + 1) * P],
+                    rhs=w1codes[:].bitcast(FP8X4),
+                    rhs_scale=w1scales[:],
+                    start=True,
+                    stop=True,
+                )
+                mv = vector_stats(y1, "l1")
+                r = inverse_deviation(mv[:, 1:2], 1, "l1")
+                nmr = small.tile([P, 1], F32, tag="l1_nmr")
+                nc.vector.scalar_tensor_tensor(
+                    out=nmr[:], in0=mv[:, 0:1], scalar=-1.0, in1=r[:], op0=ALU.mult, op1=ALU.mult
+                )
+                nc.scalar.activation(out=z[:, i, :], in_=y1[:], func=ACT.Identity, bias=nmr[:], scale=r[:])
+
+        def stage_b(p, z):
+            hp = work.tile([P, 4, 2 * P], BF16, tag="hp")
+            for half in range(2):
+                zt = psum.tile([P, D], F32, tag="zt", bufs=3)
+                for jj in range(2):
+                    j = 2 * half + jj
+                    for i in range(2):
+                        nc.tensor.transpose(
+                            out=zt[:, (2 * jj + i) * P : (2 * jj + i + 1) * P],
+                            in_=z[:, i, j * P : (j + 1) * P],
+                            identity=ident[:],
+                        )
+                for jj in range(2):
+                    j = 2 * half + jj
+                    nc.scalar.activation(
+                        out=hp[:, j, :],
+                        in_=zt[:, jj * 2 * P : (jj + 1) * 2 * P],
+                        func=ACT.Relu,
+                        bias=gb1[:, 4 + j : 5 + j],
+                        scale=gb1[:, j : j + 1],
+                    )
+            hg = work.tile([P, 2 * P, 4], BF16, align_bytes=64, tag="hg")
+            nc.vector.tensor_copy(
+                out=hg[:].rearrange("p (c i) t -> p c t i", i=4),
+                in_=hp[:].rearrange("p t (c i) -> p c t i", i=4),
+            )
+            hc = work.tile([P, 2 * P], U32, align_bytes=64, tag="hc")
+            hs = work.tile([P, 2 * P], U8, align_bytes=64, tag="hs")
+            nc.vector.quantize_mx(out=hc[:].bitcast(FP8X4), scales=hs[:], in_=hg[:].rearrange("p k t -> p (k t)"))
+            return hc, hs
+
+        def stage_c(p, hc, hs):
+            o = work.tile([P, 2, D], F32, tag="o")
+            for i in range(2):
+                y2 = psum.tile([P, D], F32, tag="y2", bufs=2)
+                nc.tensor.matmul_mx(
+                    out=y2[:],
+                    lhsT=hc[:, i * P : (i + 1) * P].bitcast(FP8X4),
+                    lhsT_scale=hs[:, i * P : (i + 1) * P],
+                    rhs=w2codes[:].bitcast(FP8X4),
+                    rhs_scale=w2scales[:],
+                    start=True,
+                    stop=True,
+                )
+                t = work.tile([P, D], F32, tag="t")
+                if p in V_STATS_PAIRS:
+                    mv = vector_stats(y2, "l2")
+                    r = inverse_deviation(mv[:, 1:2], 1, "l2")
+                    nc.vector.scalar_tensor_tensor(
+                        out=t[:], in0=y2[:], scalar=mv[:, 0:1], in1=gb2[:, 0, :], op0=ALU.subtract, op1=ALU.mult
+                    )
+                else:
+                    y2s = work.tile([P, D], F32, tag="y2s")
+                    total = small.tile([P, 1], F32, tag="l2_total")
+                    nc.scalar.activation(out=y2s[:], in_=y2[:], func=ACT.Identity, accum_out=total[:])
+                    negmu = small.tile([P, 1], F32, tag="l2_negmu")
+                    nc.scalar.mul(out=negmu[:], in_=total[:], mul=-1.0 / D)
+                    junk = work.tile([P, D], BF16, tag="junk")
+                    ssq = small.tile([P, 1], F32, tag="l2_ssq")
+                    nc.scalar.activation(out=junk[:], in_=y2s[:], func=ACT.Square, bias=negmu[:], accum_out=ssq[:])
+                    r = inverse_deviation(ssq[:], D, "l2")
+                    nc.vector.scalar_tensor_tensor(
+                        out=t[:], in0=y2s[:], scalar=negmu[:], in1=gb2[:, 0, :], op0=ALU.add, op1=ALU.mult
+                    )
+                nc.vector.scalar_tensor_tensor(
+                    out=o[:, i, :], in0=t[:], scalar=r[:], in1=gb2[:, 1, :], op0=ALU.mult, op1=ALU.add
+                )
+            nc.sync.dma_start(out=out[:, 2 * p : 2 * p + 2, :], in_=o[:])
+
+        stage_x(0)
+        stage_x(1)
+        w2codes, w2scales = quantise_weight(w2raw, "w2")
+        for p in range(N_PAIRS):
+            z = work.tile([P, 2, D], F32, tag="z")
+            stage_a(p, z)
+            if p + 2 < N_PAIRS:
+                stage_x(p + 2)
+            hc, hs = stage_b(p, z)
+            stage_c(p, hc, hs)

@@ -15,10 +15,12 @@ P = 128
 S = 16
 D = 512
 EPS = 1e-9
-N_PAIRS = S // 2
+NP = S // 2
 FLOPS = 2 * 2 * (P * S) * D * D
 
-V_STATS_PAIRS = (3, 7)
+PINNED = True
+V_STATS = (0,)
+G_FINAL = ()
 
 
 def tile_rlstmcell_pa_kernel(
@@ -28,19 +30,23 @@ def tile_rlstmcell_pa_kernel(
     with ExitStack() as ctx:
         const = ctx.enter_context(tc.tile_pool(name="const", bufs=1))
         work = ctx.enter_context(tc.tile_pool(name="work", bufs=3))
-        small = ctx.enter_context(tc.tile_pool(name="small", bufs=4))
-        psum = ctx.enter_context(tc.psum_pool(name="psum", bufs=1))
+        small = ctx.enter_context(tc.tile_pool(name="small", bufs=5))
+        psum = ctx.enter_context(tc.psum_pool(name="psum", bufs=2))
+        if PINNED:
+            ctx.enter_context(tc.manual_schedule())
 
-        warm_in = const.tile([P, 1], F32)
-        warm_out = const.tile([P, 1], F32)
-        nc.vector.memset(warm_in[:], 1.0)
-        nc.scalar.sqrt(out=warm_out[:], in_=warm_in[:])
+        def bank(tag, name):
+            return psum.tile([P, D], F32, tag=tag, bufs=(4 if tag == "zt" else 2), name=name)
+
         rows1 = const.tile([P, P], BF16)
         nc.vector.memset(rows1[:], 0.0)
         rows2 = const.tile([P, 2 * D], BF16)
         nc.vector.memset(rows2[:], 0.0)
         ones = const.tile([P, P], BF16)
         nc.vector.memset(ones[:], 1.0)
+        warm_in = const.tile([P, 1], F32)
+        warm_out = const.tile([P, 1], F32)
+        nc.vector.memset(warm_in[:], 1.0)
         ident = const.tile([P, P], F32)
         make_identity(nc, ident[:])
 
@@ -48,182 +54,391 @@ def tile_rlstmcell_pa_kernel(
         nc.scalar.dma_start(out=rows1[4:8, :], in_=mlp_bias_1.rearrange("(j c) -> j c", c=P))
         nc.scalar.dma_start(out=rows2[0:1, 0:D], in_=mlp_gain_2.rearrange("(o c) -> o c", o=1))
         nc.scalar.dma_start(out=rows2[0:1, D : 2 * D], in_=mlp_bias_2.rearrange("(o c) -> o c", o=1))
-
+        nc.scalar.sqrt(out=warm_out[:], in_=warm_in[:])
         w1raw = const.tile([P, 4, D], BF16)
         nc.sync.dma_start(
             out=w1raw[:].rearrange("q (u e) c -> q u e c", u=2),
             in_=mlp_kernel_1.rearrange("(u q e) c -> q u e c", u=2, e=2),
         )
         x_all = const.tile([P, S, D], BF16)
+        for lo, hi in ((0, 2), (2, 4), (4, 8), (8, 12), (12, 16)):
+            nc.sync.dma_start(out=x_all[:, lo:hi, :], in_=c_att[:, lo:hi, :])
         w2raw = const.tile([P, 4, D], BF16)
-        for lo, hi in ((0, 2), (2, 4), (4, 8)):
-            nc.sync.dma_start(out=x_all[:, lo:hi, :], in_=c_att[:, lo:hi, :])
         nc.sync.dma_start(out=w2raw[:], in_=mlp_kernel_2.rearrange("(j p) c -> p j c", p=P))
-        for lo, hi in ((8, 12), (12, 16)):
-            nc.sync.dma_start(out=x_all[:, lo:hi, :], in_=c_att[:, lo:hi, :])
         x_words = x_all[:].rearrange("p s d -> p (s d)").bitcast(F32)
 
+        live = {}
+
         rows1f = const.tile([P, P], F32)
-        nc.vector.tensor_copy(out=rows1f[:], in_=rows1[:])
-        gb1_ps = psum.tile([P, D], F32, tag="xt", bufs=1)
-        nc.tensor.transpose(out=gb1_ps[:, 0:P], in_=rows1f[:], identity=ident[:])
         gb1 = const.tile([P, 8], F32)
-        nc.vector.tensor_copy(out=gb1[:], in_=gb1_ps[:, 0:8])
         gb2 = const.tile([P, 2, D], F32)
-        for h in range(2):
-            gb2_ps = psum.tile([P, D], F32, tag="y2", bufs=2)
-            nc.tensor.matmul(out=gb2_ps[:], lhsT=ones[:], rhs=rows2[:, h * D : (h + 1) * D], start=True, stop=True)
-            nc.scalar.copy(out=gb2[:, h, :], in_=gb2_ps[:])
 
-        def quantise_weight(raw, label):
-            grouped = const.tile([P, D, 4], BF16, align_bytes=64, name=label + "_grouped")
-            nc.vector.tensor_copy(
-                out=grouped[:].rearrange("p (c i) t -> p c t i", i=4),
-                in_=raw[:].rearrange("p t (c i) -> p c t i", i=4),
-            )
-            codes = const.tile([P, D], U32, align_bytes=64, name=label + "_codes")
-            scales = const.tile([P, D], U8, align_bytes=64, name=label + "_scales")
-            nc.vector.quantize_mx(
-                out=codes[:].bitcast(FP8X4), scales=scales[:], in_=grouped[:].rearrange("p c t -> p (c t)")
-            )
-            return codes, scales
+        def gains1_cast():
+            nc.vector.tensor_copy(out=rows1f[:], in_=rows1[:])
 
-        w1codes, w1scales = quantise_weight(w1raw, "w1")
+        def gains1_transpose():
+            live["gb1_ps"] = bank("yn", "gb1_ps")
+            nc.tensor.transpose(out=live["gb1_ps"][:, 0:P], in_=rows1f[:], identity=ident[:])
 
+        def gains1_copy():
+            nc.vector.tensor_copy(out=gb1[:], in_=live["gb1_ps"][:, 0:8])
+
+        def gains2():
+            for h in range(2):
+                gb2_ps = bank("ys", "gb2_ps")
+                nc.tensor.matmul(out=gb2_ps[:], lhsT=ones[:], rhs=rows2[:, h * D : (h + 1) * D], start=True, stop=True)
+                nc.vector.tensor_copy(out=gb2[:, h, :], in_=gb2_ps[:])
+
+        wg = {}
+        wcodes = {}
+        wscales = {}
+        for label in ("w1", "w2"):
+            wg[label] = const.tile([P, D, 4], BF16, align_bytes=64, name=label + "_grouped")
+            wcodes[label] = const.tile([P, D], U32, align_bytes=64, name=label + "_codes")
+            wscales[label] = const.tile([P, D], U8, align_bytes=64, name=label + "_scales")
         xcodes = const.tile([P, S * P], U32, align_bytes=64)
         xscales = const.tile([P, S * P], U8, align_bytes=64)
+        hcodes = const.tile([P, S * P], U32, align_bytes=64)
+        hscales = const.tile([P, S * P], U8, align_bytes=64)
 
-        def stage_x(p):
-            xt = psum.tile([P, D], F32, tag="xt", bufs=1)
+        def regroup_weight(label, raw, lo, hi):
+            nc.vector.tensor_copy(
+                out=wg[label][:, lo:hi, :].rearrange("p (c i) t -> p c t i", i=4),
+                in_=raw[:, :, lo:hi].rearrange("p t (c i) -> p c t i", i=4),
+            )
+
+        def quantise_weight(label, lo, hi):
+            nc.vector.quantize_mx(
+                out=wcodes[label][:, lo:hi].bitcast(FP8X4),
+                scales=wscales[label][:, lo:hi],
+                in_=wg[label][:, lo:hi, :].rearrange("p c t -> p (c t)"),
+            )
+
+        def ok(q):
+            return 0 <= q < NP
+
+        def mx(dst, codes, scales, s, label):
+            nc.tensor.matmul_mx(
+                out=dst[:],
+                lhsT=codes[:, s * P : (s + 1) * P].bitcast(FP8X4),
+                lhsT_scale=scales[:, s * P : (s + 1) * P],
+                rhs=wcodes[label][:].bitcast(FP8X4),
+                rhs_scale=wscales[label][:],
+                start=True,
+                stop=True,
+            )
+
+        def XT(q):
+            if not ok(q):
+                return
+            xt = bank("zt", "xt")
+            live["xt", q] = xt
             for i in range(2):
                 for u in range(2):
-                    col = (2 * p + i) * 256 + u * P
+                    col = (2 * q + i) * 256 + u * P
                     nc.tensor.transpose(
                         out=xt[:, (2 * i + u) * P : (2 * i + u + 1) * P],
                         in_=x_words[:, col : col + P],
                         identity=ident[:],
                     )
-            xg = work.tile([P, 2 * D], BF16, align_bytes=64, tag="xg")
+
+        def XC(q):
+            if not ok(q):
+                return
+            xg = work.tile([P, 2 * D], BF16, align_bytes=64, tag="xg", bufs=4, name="xg")
+            live["xg", q] = xg
             nc.scalar.copy(
                 out=xg[:].bitcast(F32).rearrange("p (i k u) -> p i k u", i=2, u=2),
-                in_=xt[:].rearrange("p (i u k) -> p i k u", i=2, u=2),
+                in_=live["xt", q][:].rearrange("p (i u k) -> p i k u", i=2, u=2),
             )
-            cols = slice(2 * p * P, (2 * p + 2) * P)
-            nc.vector.quantize_mx(out=xcodes[:, cols].bitcast(FP8X4), scales=xscales[:, cols], in_=xg[:])
 
-        def inverse_deviation(sum_ap, divisor, label):
-            sd = small.tile([P, 1], F32, tag=label + "_sd")
-            nc.scalar.activation(out=sd[:], in_=sum_ap, func=ACT.Sqrt, scale=1.0 / divisor)
-            sde = small.tile([P, 1], F32, tag=label + "_sde")
-            nc.vector.tensor_scalar_add(out=sde[:], in0=sd[:], scalar1=EPS)
-            r = small.tile([P, 1], F32, tag=label + "_r")
-            nc.vector.reciprocal(out=r[:], in_=sde[:])
-            return r
+        def XQ(q):
+            if not ok(q):
+                return
+            cols = slice(2 * q * P, (2 * q + 2) * P)
+            nc.vector.quantize_mx(out=xcodes[:, cols].bitcast(FP8X4), scales=xscales[:, cols], in_=live["xg", q][:])
 
-        def vector_stats(y, label):
-            st = small.tile([P, 6], F32, tag=label + "_st")
-            nc.vector.bn_stats(out=st[:], in_=y[:])
-            mv = small.tile([P, 2], F32, tag=label + "_mv")
-            nc.vector.bn_aggr(out=mv[:], in_=st[:])
-            return mv
-
-        def stage_a(p, z):
+        def MS(q):
+            if not ok(q):
+                return
             for i in range(2):
-                s = 2 * p + i
-                y1 = psum.tile([P, D], F32, tag="y1", bufs=2)
-                nc.tensor.matmul_mx(
-                    out=y1[:],
-                    lhsT=xcodes[:, s * P : (s + 1) * P].bitcast(FP8X4),
-                    lhsT_scale=xscales[:, s * P : (s + 1) * P],
-                    rhs=w1codes[:].bitcast(FP8X4),
-                    rhs_scale=w1scales[:],
-                    start=True,
-                    stop=True,
-                )
-                mv = vector_stats(y1, "l1")
-                r = inverse_deviation(mv[:, 1:2], 1, "l1")
-                nmr = small.tile([P, 1], F32, tag="l1_nmr")
-                nc.vector.scalar_tensor_tensor(
-                    out=nmr[:], in0=mv[:, 0:1], scalar=-1.0, in1=r[:], op0=ALU.mult, op1=ALU.mult
-                )
-                nc.scalar.activation(out=z[:, i, :], in_=y1[:], func=ACT.Identity, bias=nmr[:], scale=r[:])
+                live["ys", q, i] = bank("ys", "ys")
+                mx(live["ys", q, i], xcodes, xscales, 2 * q + i, "w1")
 
-        def stage_b(p, z):
-            hp = work.tile([P, 4, 2 * P], BF16, tag="hp")
-            for half in range(2):
-                zt = psum.tile([P, D], F32, tag="zt", bufs=3)
-                for jj in range(2):
-                    j = 2 * half + jj
-                    for i in range(2):
-                        nc.tensor.transpose(
-                            out=zt[:, (2 * jj + i) * P : (2 * jj + i + 1) * P],
-                            in_=z[:, i, j * P : (j + 1) * P],
-                            identity=ident[:],
-                        )
-                for jj in range(2):
-                    j = 2 * half + jj
-                    nc.scalar.activation(
-                        out=hp[:, j, :],
-                        in_=zt[:, jj * 2 * P : (jj + 1) * 2 * P],
-                        func=ACT.Relu,
-                        bias=gb1[:, 4 + j : 5 + j],
-                        scale=gb1[:, j : j + 1],
+        def MN(q):
+            if not ok(q):
+                return
+            for i in range(2):
+                live["yn", q, i] = bank("yn", "yn")
+                mx(live["yn", q, i], xcodes, xscales, 2 * q + i, "w1")
+
+        def stats(key, q, src):
+            st = small.tile([P, 2, 6], F32, tag=key + "st", name=key + "st")
+            mv = small.tile([P, 2, 2], F32, tag=key + "mv", name=key + "mv")
+            live[key + "mv", q] = mv
+            for i in range(2):
+                nc.vector.bn_stats(out=st[:, i, :], in_=live[src, q, i][:])
+            for i in range(2):
+                nc.vector.bn_aggr(out=mv[:, i, :], in_=st[:, i, :])
+
+        def BN(q):
+            if ok(q):
+                stats("a", q, "ys")
+
+        def root(key, q, src_ap, divisor):
+            sd = small.tile([P, 2], F32, tag=key + "sd", name=key + "sd")
+            live[key + "sd", q] = sd
+            nc.scalar.activation(out=sd[:], in_=src_ap, func=ACT.Sqrt, scale=1.0 / divisor)
+
+        def add_eps(key, q):
+            sde = small.tile([P, 2], F32, tag=key + "sde", name=key + "sde")
+            live[key + "sde", q] = sde
+            nc.vector.tensor_scalar_add(out=sde[:], in0=live[key + "sd", q][:], scalar1=EPS)
+
+        def invert(key, q):
+            r = small.tile([P, 2], F32, tag=key + "r", name=key + "r")
+            live[key + "r", q] = r
+            nc.vector.reciprocal(out=r[:], in_=live[key + "sde", q][:])
+
+        def SQ(q):
+            if ok(q):
+                root("a", q, live["amv", q][:, :, 1], 1)
+
+        def E1(q):
+            if ok(q):
+                add_eps("a", q)
+
+        def R1(q):
+            if ok(q):
+                invert("a", q)
+
+        def N1(q):
+            if not ok(q):
+                return
+            nmr = small.tile([P, 2], F32, tag="anmr", name="anmr")
+            live["anmr", q] = nmr
+            nc.vector.scalar_tensor_tensor(
+                out=nmr[:], in0=live["amv", q][:, :, 0], scalar=-1.0, in1=live["ar", q][:], op0=ALU.mult, op1=ALU.mult
+            )
+
+        def NR(q):
+            if not ok(q):
+                return
+            z = work.tile([P, 2, D], F32, tag="z", name="z")
+            live["z", q] = z
+            for i in range(2):
+                nc.scalar.activation(
+                    out=z[:, i, :],
+                    in_=live["yn", q, i][:],
+                    func=ACT.Identity,
+                    bias=live["anmr", q][:, i : i + 1],
+                    scale=live["ar", q][:, i : i + 1],
+                )
+
+        def ZT(q):
+            if not ok(q):
+                return
+            zts = [bank("zt", "zt"), bank("zt", "zt")]
+            live["zt", q] = zts
+            for i in range(2):
+                for j in range(4):
+                    col = (2 * (j % 2) + i) * P
+                    nc.tensor.transpose(
+                        out=zts[j // 2][:, col : col + P],
+                        in_=live["z", q][:, i, j * P : (j + 1) * P],
+                        identity=ident[:],
                     )
-            hg = work.tile([P, 2 * P, 4], BF16, align_bytes=64, tag="hg")
+
+        def RL(q, js):
+            if not ok(q):
+                return
+            if js[0] == 0:
+                live["hp", q] = work.tile([P, 4, 2 * P], BF16, tag="hp", name="hp")
+            for j in js:
+                nc.scalar.activation(
+                    out=live["hp", q][:, j, :],
+                    in_=live["zt", q][j // 2][:, (j % 2) * 2 * P : (j % 2 + 1) * 2 * P],
+                    func=ACT.Relu,
+                    bias=gb1[:, 4 + j : 5 + j],
+                    scale=gb1[:, j : j + 1],
+                )
+
+        def RG(q):
+            if not ok(q):
+                return
+            hg = work.tile([P, 2 * P, 4], BF16, align_bytes=64, tag="hg", name="hg")
+            live["hg", q] = hg
             nc.vector.tensor_copy(
                 out=hg[:].rearrange("p (c i) t -> p c t i", i=4),
-                in_=hp[:].rearrange("p t (c i) -> p c t i", i=4),
+                in_=live["hp", q][:].rearrange("p t (c i) -> p c t i", i=4),
             )
-            hc = work.tile([P, 2 * P], U32, align_bytes=64, tag="hc")
-            hs = work.tile([P, 2 * P], U8, align_bytes=64, tag="hs")
-            nc.vector.quantize_mx(out=hc[:].bitcast(FP8X4), scales=hs[:], in_=hg[:].rearrange("p k t -> p (k t)"))
-            return hc, hs
 
-        def stage_c(p, hc, hs):
-            o = work.tile([P, 2, D], F32, tag="o")
+        def HQ(q):
+            if not ok(q):
+                return
+            cols = slice(2 * q * P, (2 * q + 2) * P)
+            nc.vector.quantize_mx(
+                out=hcodes[:, cols].bitcast(FP8X4),
+                scales=hscales[:, cols],
+                in_=live["hg", q][:].rearrange("p k t -> p (k t)"),
+            )
+
+        def M2(q):
+            if not ok(q):
+                return
+            tag = ("ys", "yn", "zt", "zt")[q % 4]
             for i in range(2):
-                y2 = psum.tile([P, D], F32, tag="y2", bufs=2)
-                nc.tensor.matmul_mx(
-                    out=y2[:],
-                    lhsT=hc[:, i * P : (i + 1) * P].bitcast(FP8X4),
-                    lhsT_scale=hs[:, i * P : (i + 1) * P],
-                    rhs=w2codes[:].bitcast(FP8X4),
-                    rhs_scale=w2scales[:],
-                    start=True,
-                    stop=True,
-                )
-                t = work.tile([P, D], F32, tag="t")
-                if p in V_STATS_PAIRS:
-                    mv = vector_stats(y2, "l2")
-                    r = inverse_deviation(mv[:, 1:2], 1, "l2")
-                    nc.vector.scalar_tensor_tensor(
-                        out=t[:], in0=y2[:], scalar=mv[:, 0:1], in1=gb2[:, 0, :], op0=ALU.subtract, op1=ALU.mult
-                    )
-                else:
-                    y2s = work.tile([P, D], F32, tag="y2s")
-                    total = small.tile([P, 1], F32, tag="l2_total")
-                    nc.scalar.activation(out=y2s[:], in_=y2[:], func=ACT.Identity, accum_out=total[:])
-                    negmu = small.tile([P, 1], F32, tag="l2_negmu")
-                    nc.scalar.mul(out=negmu[:], in_=total[:], mul=-1.0 / D)
-                    junk = work.tile([P, D], BF16, tag="junk")
-                    ssq = small.tile([P, 1], F32, tag="l2_ssq")
-                    nc.scalar.activation(out=junk[:], in_=y2s[:], func=ACT.Square, bias=negmu[:], accum_out=ssq[:])
-                    r = inverse_deviation(ssq[:], D, "l2")
-                    nc.vector.scalar_tensor_tensor(
-                        out=t[:], in0=y2s[:], scalar=negmu[:], in1=gb2[:, 0, :], op0=ALU.add, op1=ALU.mult
-                    )
-                nc.vector.scalar_tensor_tensor(
-                    out=o[:, i, :], in0=t[:], scalar=r[:], in1=gb2[:, 1, :], op0=ALU.mult, op1=ALU.add
-                )
-            nc.sync.dma_start(out=out[:, 2 * p : 2 * p + 2, :], in_=o[:])
+                live["y2", q, i] = bank(tag, "y2")
+                mx(live["y2", q, i], hcodes, hscales, 2 * q + i, "w2")
 
-        stage_x(0)
-        stage_x(1)
-        w2codes, w2scales = quantise_weight(w2raw, "w2")
-        for p in range(N_PAIRS):
-            z = work.tile([P, 2, D], F32, tag="z")
-            stage_a(p, z)
-            if p + 2 < N_PAIRS:
-                stage_x(p + 2)
-            hc, hs = stage_b(p, z)
-            stage_c(p, hc, hs)
+        def PA(q, i):
+            if not ok(q) or q in V_STATS:
+                return
+            if i == 0:
+                live["y2s", q] = work.tile([P, 2, D], F32, tag="y2s", name="y2s")
+                live["tot", q] = small.tile([P, 2], F32, tag="tot", name="tot")
+            nc.scalar.activation(
+                out=live["y2s", q][:, i, :],
+                in_=live["y2", q, i][:],
+                func=ACT.Identity,
+                accum_out=live["tot", q][:, i : i + 1],
+            )
+
+        def MU(q):
+            if not ok(q) or q in V_STATS:
+                return
+            negmu = small.tile([P, 2], F32, tag="negmu", name="negmu")
+            live["negmu", q] = negmu
+            nc.scalar.mul(out=negmu[:], in_=live["tot", q][:], mul=-1.0 / D)
+
+        def PB(q):
+            if not ok(q) or q in V_STATS:
+                return
+            ssq = small.tile([P, 2], F32, tag="ssq", name="ssq")
+            live["ssq", q] = ssq
+            for i in range(2):
+                junk = work.tile([P, D], BF16, tag="junk", bufs=2, name="junk")
+                nc.scalar.activation(
+                    out=junk[:],
+                    in_=live["y2s", q][:, i, :],
+                    func=ACT.Square,
+                    bias=live["negmu", q][:, i : i + 1],
+                    accum_out=ssq[:, i : i + 1],
+                )
+
+        def B2(q):
+            if ok(q) and q in V_STATS:
+                stats("b", q, "y2")
+
+        def S2(q):
+            if not ok(q):
+                return
+            if q in V_STATS:
+                root("b", q, live["bmv", q][:, :, 1], 1)
+            else:
+                root("b", q, live["ssq", q][:], D)
+
+        def E2(q):
+            if ok(q):
+                add_eps("b", q)
+
+        def R2(q):
+            if ok(q):
+                invert("b", q)
+
+        def T1(q, i):
+            if not ok(q):
+                return
+            if i == 0:
+                live["t", q] = work.tile([P, 2, D], F32, tag="t", name="t")
+            if q in V_STATS:
+                nc.vector.scalar_tensor_tensor(
+                    out=live["t", q][:, i, :],
+                    in0=live["y2", q, i][:],
+                    scalar=live["bmv", q][:, i, 0:1],
+                    in1=gb2[:, 0, :],
+                    op0=ALU.subtract,
+                    op1=ALU.mult,
+                )
+            else:
+                nc.vector.scalar_tensor_tensor(
+                    out=live["t", q][:, i, :],
+                    in0=live["y2s", q][:, i, :],
+                    scalar=live["negmu", q][:, i : i + 1],
+                    in1=gb2[:, 0, :],
+                    op0=ALU.add,
+                    op1=ALU.mult,
+                )
+
+        def T2(q):
+            if not ok(q):
+                return
+            o = work.tile([P, 2, D], F32, tag="o", bufs=4, name="o")
+            for i in range(2):
+                r = live["br", q][:, i : i + 1]
+                if q in G_FINAL:
+                    u = work.tile([P, D], F32, tag="u", name="u")
+                    nc.gpsimd.tensor_scalar(
+                        out=u[:], in0=live["t", q][:, i, :], scalar1=r, scalar2=0.0, op0=ALU.mult, op1=ALU.add
+                    )
+                    nc.gpsimd.tensor_tensor(out=o[:, i, :], in0=u[:], in1=gb2[:, 1, :], op=ALU.add)
+                else:
+                    nc.vector.scalar_tensor_tensor(
+                        out=o[:, i, :], in0=live["t", q][:, i, :], scalar=r, in1=gb2[:, 1, :], op0=ALU.mult, op1=ALU.add
+                    )
+                if q == NP - 1:
+                    nc.sync.dma_start(out=out[:, 2 * q + i, :], in_=o[:, i, :])
+            if q < NP - 1:
+                nc.sync.dma_start(out=out[:, 2 * q : 2 * q + 2, :], in_=o[:])
+
+        regroup_weight("w1", w1raw, 0, 256)
+        regroup_weight("w1", w1raw, 256, 512)
+        quantise_weight("w1", 0, 256)
+        quantise_weight("w1", 256, 512)
+        XT(0), XC(0), XT(1), XC(1), XQ(0), MS(0), XQ(1), gains1_cast(), gains1_transpose()
+        XT(2), XC(2), XT(3), XC(3), BN(0), gains1_copy(), MN(0)
+        MS(1), SQ(0), XQ(2), E1(0), XQ(3), R1(0), XT(4), XT(5), XT(6), XT(7), N1(0)
+        NR(0), BN(1), MS(2), MN(1), XC(4), SQ(1), BN(2), XC(5), ZT(0), MS(3), XC(6), XC(7), SQ(2)
+        E1(1), XQ(4), R1(1), XQ(5), N1(1)
+        for n in range(1, NP + 3):
+            NR(n), MN(n + 1), ZT(n)
+            BN(n + 2), MS(n + 3), E1(n + 1)
+            if n == 1:
+                XQ(6)
+            RG(n - 2), R1(n + 1)
+            if n == 1:
+                XQ(7)
+            HQ(n - 3), N1(n + 1)
+            if n == 6:
+                regroup_weight("w2", w2raw, 0, 512)
+                gains2()
+            if n == 7:
+                quantise_weight("w2", 0, 512)
+                M2(0), B2(0)
+            RL(n - 1, (0, 1)), SQ(n + 2)
+            if n == 8:
+                S2(0)
+            RL(n - 1, (2, 3))
+            if n == 8:
+                M2(1), T1(0, 0), E2(0), T1(0, 1), R2(0)
+            if n == 9:
+                T2(0)
+        M2(2), M2(3), M2(4)
+        for k in range(1, NP + 3):
+            PA(k, 0)
+            if k >= 3:
+                S2(k - 2)
+            PA(k, 1), M2(k + 4)
+            if k >= 2:
+                PB(k - 1)
+            MU(k)
+            if k >= 3:
+                E2(k - 2)
+            if k >= 2:
+                T1(k - 1, 0)
+            if k >= 3:
+                R2(k - 2)
+            if k >= 2:
+                T1(k - 1, 1)
+            if k >= 3:
+                T2(k - 2)

@@ -20,7 +20,6 @@ FLOPS = 2 * 2 * (P * S) * D * D
 
 PINNED = True
 V_STATS = (0,)
-G_FINAL = ()
 
 
 def tile_rlstmcell_pa_kernel(
@@ -158,32 +157,33 @@ def tile_rlstmcell_pa_kernel(
             cols = slice(2 * q * P, (2 * q + 2) * P)
             nc.vector.quantize_mx(out=xcodes[:, cols].bitcast(FP8X4), scales=xscales[:, cols], in_=live["xg", q][:])
 
-        def MS(q):
-            if not ok(q):
-                return
-            for i in range(2):
+        def MS(q, i):
+            if ok(q):
                 live["ys", q, i] = bank("ys", "ys")
                 mx(live["ys", q, i], xcodes, xscales, 2 * q + i, "w1")
 
-        def MN(q):
-            if not ok(q):
-                return
-            for i in range(2):
+        def MN(q, i):
+            if ok(q):
                 live["yn", q, i] = bank("yn", "yn")
                 mx(live["yn", q, i], xcodes, xscales, 2 * q + i, "w1")
 
-        def stats(key, q, src):
-            st = small.tile([P, 2, 6], F32, tag=key + "st", name=key + "st")
-            mv = small.tile([P, 2, 2], F32, tag=key + "mv", name=key + "mv")
-            live[key + "mv", q] = mv
-            for i in range(2):
-                nc.vector.bn_stats(out=st[:, i, :], in_=live[src, q, i][:])
-            for i in range(2):
-                nc.vector.bn_aggr(out=mv[:, i, :], in_=st[:, i, :])
+        def moments(key, q, i, src):
+            if i == 0:
+                live[key + "st", q] = small.tile([P, 2, 6], F32, tag=key + "st", name=key + "st")
+            nc.vector.bn_stats(out=live[key + "st", q][:, i, :], in_=live[src, q, i][:])
 
-        def BN(q):
+        def aggregate(key, q, i):
+            if i == 0:
+                live[key + "mv", q] = small.tile([P, 2, 2], F32, tag=key + "mv", name=key + "mv")
+            nc.vector.bn_aggr(out=live[key + "mv", q][:, i, :], in_=live[key + "st", q][:, i, :])
+
+        def BN(q, i):
             if ok(q):
-                stats("a", q, "ys")
+                moments("a", q, i, "ys")
+
+        def AG(q, i):
+            if ok(q):
+                aggregate("a", q, i)
 
         def root(key, q, src_ap, divisor):
             sd = small.tile([P, 2], F32, tag=key + "sd", name=key + "sd")
@@ -221,19 +221,18 @@ def tile_rlstmcell_pa_kernel(
                 out=nmr[:], in0=live["amv", q][:, :, 0], scalar=-1.0, in1=live["ar", q][:], op0=ALU.mult, op1=ALU.mult
             )
 
-        def NR(q):
+        def NR(q, i):
             if not ok(q):
                 return
-            z = work.tile([P, 2, D], F32, tag="z", name="z")
-            live["z", q] = z
-            for i in range(2):
-                nc.scalar.activation(
-                    out=z[:, i, :],
-                    in_=live["yn", q, i][:],
-                    func=ACT.Identity,
-                    bias=live["anmr", q][:, i : i + 1],
-                    scale=live["ar", q][:, i : i + 1],
-                )
+            if i == 0:
+                live["z", q] = work.tile([P, 2, D], F32, tag="z", name="z")
+            nc.scalar.activation(
+                out=live["z", q][:, i, :],
+                in_=live["yn", q, i][:],
+                func=ACT.Identity,
+                bias=live["anmr", q][:, i : i + 1],
+                scale=live["ar", q][:, i : i + 1],
+            )
 
         def ZT(q):
             if not ok(q):
@@ -326,9 +325,13 @@ def tile_rlstmcell_pa_kernel(
                     accum_out=ssq[:, i : i + 1],
                 )
 
-        def B2(q):
+        def B2(q, i):
             if ok(q) and q in V_STATS:
-                stats("b", q, "y2")
+                moments("b", q, i, "y2")
+
+        def A2(q, i):
+            if ok(q) and q in V_STATS:
+                aggregate("b", q, i)
 
         def S2(q):
             if not ok(q):
@@ -370,75 +373,64 @@ def tile_rlstmcell_pa_kernel(
                     op1=ALU.mult,
                 )
 
-        def T2(q):
+        def T2(q, i):
             if not ok(q):
                 return
-            o = work.tile([P, 2, D], F32, tag="o", bufs=4, name="o")
-            for i in range(2):
-                r = live["br", q][:, i : i + 1]
-                if q in G_FINAL:
-                    u = work.tile([P, D], F32, tag="u", name="u")
-                    nc.gpsimd.tensor_scalar(
-                        out=u[:], in0=live["t", q][:, i, :], scalar1=r, scalar2=0.0, op0=ALU.mult, op1=ALU.add
-                    )
-                    nc.gpsimd.tensor_tensor(out=o[:, i, :], in0=u[:], in1=gb2[:, 1, :], op=ALU.add)
-                else:
-                    nc.vector.scalar_tensor_tensor(
-                        out=o[:, i, :], in0=live["t", q][:, i, :], scalar=r, in1=gb2[:, 1, :], op0=ALU.mult, op1=ALU.add
-                    )
-                if q == NP - 1:
-                    nc.sync.dma_start(out=out[:, 2 * q + i, :], in_=o[:, i, :])
-            if q < NP - 1:
+            if i == 0:
+                live["o", q] = work.tile([P, 2, D], F32, tag="o", bufs=4, name="o")
+            o = live["o", q]
+            nc.vector.scalar_tensor_tensor(
+                out=o[:, i, :],
+                in0=live["t", q][:, i, :],
+                scalar=live["br", q][:, i : i + 1],
+                in1=gb2[:, 1, :],
+                op0=ALU.mult,
+                op1=ALU.add,
+            )
+            if q == NP - 1:
+                nc.sync.dma_start(out=out[:, 2 * q + i, :], in_=o[:, i, :])
+            elif i == 1:
                 nc.sync.dma_start(out=out[:, 2 * q : 2 * q + 2, :], in_=o[:])
 
         regroup_weight("w1", w1raw, 0, 256)
         regroup_weight("w1", w1raw, 256, 512)
         quantise_weight("w1", 0, 256)
         quantise_weight("w1", 256, 512)
-        XT(0), XC(0), XT(1), XC(1), XQ(0), MS(0), XQ(1), gains1_cast(), gains1_transpose()
-        XT(2), XC(2), XT(3), XC(3), BN(0), gains1_copy(), MN(0)
-        MS(1), SQ(0), XQ(2), E1(0), XQ(3), R1(0), XT(4), XT(5), XT(6), XT(7), N1(0)
-        NR(0), BN(1), MS(2), MN(1), XC(4), SQ(1), BN(2), XC(5), ZT(0), MS(3), XC(6), XC(7), SQ(2)
-        E1(1), XQ(4), R1(1), XQ(5), N1(1)
+        XT(0), XC(0), XT(1), XC(1), XQ(0), XT(2), XC(2), XT(3), XC(3), MS(0, 0), MS(0, 1), XQ(1)
+        XT(4), XC(4), XT(5), XC(5)
+        BN(0, 0), BN(0, 1), gains1_cast(), XT(6), XT(7), gains1_transpose(), MS(1, 0), MS(1, 1)
+        XQ(2), AG(0, 0), XQ(3), AG(0, 1), SQ(0), XC(6)
+        BN(1, 0), E1(0), BN(1, 1), gains1_copy(), MS(2, 0), MS(2, 1), MN(0, 0), MN(0, 1), R1(0), AG(1, 0), XQ(4), AG(1, 1), N1(0)
+        XC(7), SQ(1)
+        BN(2, 0), BN(2, 1), MS(3, 0), MS(3, 1), E1(1), AG(2, 0), R1(1), AG(2, 1), N1(1)
+        NR(0, 0), NR(0, 1), SQ(2), MN(1, 0), MN(1, 1), ZT(0)
         for n in range(1, NP + 3):
-            NR(n), MN(n + 1), ZT(n)
-            BN(n + 2), MS(n + 3), E1(n + 1)
-            if n == 1:
-                XQ(6)
-            RG(n - 2), R1(n + 1)
-            if n == 1:
-                XQ(7)
-            HQ(n - 3), N1(n + 1)
+            NR(n, 0), NR(n, 1)
+            BN(n + 2, 0), MS(n + 3, 0), MN(n + 1, 0), MN(n + 1, 1), E1(n + 1), BN(n + 2, 1), MS(n + 3, 1), ZT(n)
+            AG(n + 2, 0), R1(n + 1)
+            if n <= 3:
+                XQ(n + 4)
+            RG(n - 2), AG(n + 2, 1), HQ(n - 3), N1(n + 1)
+            RL(n - 1, (0, 1, 2, 3)), SQ(n + 2)
             if n == 6:
                 regroup_weight("w2", w2raw, 0, 512)
                 gains2()
             if n == 7:
                 quantise_weight("w2", 0, 512)
-                M2(0), B2(0)
-            RL(n - 1, (0, 1)), SQ(n + 2)
+                M2(0), B2(0, 0), B2(0, 1), A2(0, 0)
             if n == 8:
-                S2(0)
-            RL(n - 1, (2, 3))
-            if n == 8:
-                M2(1), T1(0, 0), E2(0), T1(0, 1), R2(0)
-            if n == 9:
-                T2(0)
+                M2(1), A2(0, 1), T1(0, 0), T1(0, 1)
         M2(2), M2(3), M2(4)
-        for k in range(1, NP + 3):
-            PA(k, 0)
-            if k >= 3:
-                S2(k - 2)
-            PA(k, 1), M2(k + 4)
+        for k in range(1, NP + 1):
+            PA(k, 0), S2(k - 2), PA(k, 1), M2(k + 4)
             if k >= 2:
                 PB(k - 1)
-            MU(k)
-            if k >= 3:
-                E2(k - 2)
+            MU(k), E2(k - 2)
             if k >= 2:
                 T1(k - 1, 0)
-            if k >= 3:
-                R2(k - 2)
+            R2(k - 2)
             if k >= 2:
                 T1(k - 1, 1)
-            if k >= 3:
-                T2(k - 2)
+            if k < NP:
+                T2(k - 2, 0), T2(k - 2, 1)
+        S2(NP - 1), E2(NP - 1), T2(NP - 2, 0), R2(NP - 1), T2(NP - 2, 1), T2(NP - 1, 0), T2(NP - 1, 1)

@@ -19,7 +19,7 @@ NP = S // 2
 FLOPS = 2 * 2 * (P * S) * D * D
 
 PINNED = True
-V_STATS = (0,)
+V_STATS = (0, 1)
 
 
 def tile_rlstmcell_pa_kernel(
@@ -39,10 +39,6 @@ def tile_rlstmcell_pa_kernel(
 
         rows1 = const.tile([P, P], BF16)
         nc.vector.memset(rows1[:], 0.0)
-        rows2 = const.tile([P, 2 * D], BF16)
-        nc.vector.memset(rows2[:], 0.0)
-        ones = const.tile([P, P], BF16)
-        nc.vector.memset(ones[:], 1.0)
         warm_in = const.tile([P, 1], F32)
         warm_out = const.tile([P, 1], F32)
         nc.vector.memset(warm_in[:], 1.0)
@@ -51,8 +47,6 @@ def tile_rlstmcell_pa_kernel(
 
         nc.scalar.dma_start(out=rows1[0:4, :], in_=mlp_gain_1.rearrange("(j c) -> j c", c=P))
         nc.scalar.dma_start(out=rows1[4:8, :], in_=mlp_bias_1.rearrange("(j c) -> j c", c=P))
-        nc.scalar.dma_start(out=rows2[0:1, 0:D], in_=mlp_gain_2.rearrange("(o c) -> o c", o=1))
-        nc.scalar.dma_start(out=rows2[0:1, D : 2 * D], in_=mlp_bias_2.rearrange("(o c) -> o c", o=1))
         nc.scalar.sqrt(out=warm_out[:], in_=warm_in[:])
         w1raw = const.tile([P, 4, D], BF16)
         nc.sync.dma_start(
@@ -64,13 +58,15 @@ def tile_rlstmcell_pa_kernel(
             nc.sync.dma_start(out=x_all[:, lo:hi, :], in_=c_att[:, lo:hi, :])
         w2raw = const.tile([P, 4, D], BF16)
         nc.sync.dma_start(out=w2raw[:], in_=mlp_kernel_2.rearrange("(j p) c -> p j c", p=P))
+        gb2 = const.tile([P, 2, D], BF16)
+        nc.sync.dma_start(out=gb2[:, 0, :], in_=mlp_gain_2.partition_broadcast(P))
+        nc.sync.dma_start(out=gb2[:, 1, :], in_=mlp_bias_2.partition_broadcast(P))
         x_words = x_all[:].rearrange("p s d -> p (s d)").bitcast(F32)
 
         live = {}
 
         rows1f = const.tile([P, P], F32)
         gb1 = const.tile([P, 8], F32)
-        gb2 = const.tile([P, 2, D], F32)
 
         def gains1_cast():
             nc.vector.tensor_copy(out=rows1f[:], in_=rows1[:])
@@ -81,12 +77,6 @@ def tile_rlstmcell_pa_kernel(
 
         def gains1_copy():
             nc.vector.tensor_copy(out=gb1[:], in_=live["gb1_ps"][:, 0:8])
-
-        def gains2():
-            for h in range(2):
-                gb2_ps = bank("ys", "gb2_ps")
-                nc.tensor.matmul(out=gb2_ps[:], lhsT=ones[:], rhs=rows2[:, h * D : (h + 1) * D], start=True, stop=True)
-                nc.vector.tensor_copy(out=gb2[:, h, :], in_=gb2_ps[:])
 
         wg = {}
         wcodes = {}
@@ -285,7 +275,7 @@ def tile_rlstmcell_pa_kernel(
         def M2(q):
             if not ok(q):
                 return
-            tag = ("ys", "yn", "zt", "zt")[q % 4]
+            tag = ("ys", "ys", "yn", "zt", "zt", "ys", "yn", "zt")[q]
             for i in range(2):
                 live["y2", q, i] = bank(tag, "y2")
                 mx(live["y2", q, i], hcodes, hscales, 2 * q + i, "w2")
@@ -392,45 +382,79 @@ def tile_rlstmcell_pa_kernel(
             elif i == 1:
                 nc.sync.dma_start(out=out[:, 2 * q : 2 * q + 2, :], in_=o[:])
 
+        def late(n, i):
+            u = n - 6
+            if 0 <= u <= 3:
+                if u % 2 == 0:
+                    B2(u // 2, i)
+                else:
+                    T1(u // 2, i)
+
         regroup_weight("w1", w1raw, 0, 256)
         regroup_weight("w1", w1raw, 256, 512)
         quantise_weight("w1", 0, 256)
         quantise_weight("w1", 256, 512)
         XT(0), XC(0), XT(1), XC(1), XQ(0), XT(2), XC(2), XT(3), XC(3), MS(0, 0), MS(0, 1), XQ(1)
         XT(4), XC(4), XT(5), XC(5)
-        BN(0, 0), BN(0, 1), gains1_cast(), XT(6), XT(7), gains1_transpose(), MS(1, 0), MS(1, 1)
+        BN(0, 0), BN(0, 1), gains1_cast(), MS(1, 0), MS(1, 1), XT(6), XT(7), gains1_transpose()
         XQ(2), AG(0, 0), XQ(3), AG(0, 1), SQ(0), XC(6)
-        BN(1, 0), E1(0), BN(1, 1), gains1_copy(), MS(2, 0), MS(2, 1), MN(0, 0), MN(0, 1), R1(0), AG(1, 0), XQ(4), AG(1, 1), N1(0)
-        XC(7), SQ(1)
-        BN(2, 0), BN(2, 1), MS(3, 0), MS(3, 1), E1(1), AG(2, 0), R1(1), AG(2, 1), N1(1)
+        BN(1, 0), E1(0), gains1_copy(), MN(0, 0), MN(0, 1), BN(1, 1), MS(2, 0), MS(2, 1)
+        R1(0), AG(1, 0), XQ(4), AG(1, 1), N1(0), XC(7), SQ(1)
+        BN(2, 0), BN(2, 1), MS(3, 0), MS(3, 1), E1(1), AG(2, 0)
+        regroup_weight("w2", w2raw, 0, 128)
+        R1(1), AG(2, 1)
+        regroup_weight("w2", w2raw, 128, 256)
+        N1(1)
         NR(0, 0), NR(0, 1), SQ(2), MN(1, 0), MN(1, 1), ZT(0)
         for n in range(1, NP + 3):
             NR(n, 0), NR(n, 1)
-            BN(n + 2, 0), MS(n + 3, 0), MN(n + 1, 0), MN(n + 1, 1), E1(n + 1), BN(n + 2, 1), MS(n + 3, 1), ZT(n)
-            AG(n + 2, 0), R1(n + 1)
+            BN(n + 2, 0), late(n, 0), MS(n + 3, 0), MN(n + 1, 0), MN(n + 1, 1), E1(n + 1)
+            if n == 8:
+                E2(0)
+            BN(n + 2, 1), late(n, 1), MS(n + 3, 1)
+            if n == 5:
+                M2(0)
+            if n == 7:
+                M2(1)
+            ZT(n), R1(n + 1)
+            if n == 8:
+                R2(0)
+            RG(n - 2)
+            if n == 1:
+                regroup_weight("w2", w2raw, 256, 384)
+            AG(n + 2, 0), AG(n + 2, 1)
+            if n == 6 or n == 8:
+                A2((n - 6) // 2, 0), A2((n - 6) // 2, 1)
+            N1(n + 1), HQ(n - 3)
             if n <= 3:
                 XQ(n + 4)
-            RG(n - 2), AG(n + 2, 1), HQ(n - 3), N1(n + 1)
+            if n == 2:
+                regroup_weight("w2", w2raw, 384, 512)
+            if n == 3:
+                quantise_weight("w2", 0, 256)
+            if n == 4:
+                quantise_weight("w2", 256, 512)
+            if n == 9:
+                T2(0, 0), T2(0, 1)
             RL(n - 1, (0, 1, 2, 3)), SQ(n + 2)
-            if n == 6:
-                regroup_weight("w2", w2raw, 0, 512)
-                gains2()
             if n == 7:
-                quantise_weight("w2", 0, 512)
-                M2(0), B2(0, 0), B2(0, 1), A2(0, 0)
+                S2(0), M2(2)
             if n == 8:
-                M2(1), A2(0, 1), T1(0, 0), T1(0, 1)
-        M2(2), M2(3), M2(4)
-        for k in range(1, NP + 1):
-            PA(k, 0), S2(k - 2), PA(k, 1), M2(k + 4)
-            if k >= 2:
-                PB(k - 1)
-            MU(k), E2(k - 2)
-            if k >= 2:
-                T1(k - 1, 0)
-            R2(k - 2)
-            if k >= 2:
-                T1(k - 1, 1)
-            if k < NP:
-                T2(k - 2, 0), T2(k - 2, 1)
+                M2(3), M2(4)
+            if n == 9:
+                M2(5)
+        for k in range(2, NP + 1):
+            PA(k, 0)
+            if k == 3:
+                MU(2)
+            if k >= 3:
+                S2(k - 2)
+            PA(k, 1)
+            if k <= 3:
+                M2(k + 4)
+            if k >= 3:
+                PB(k - 1), MU(k)
+                E2(k - 2), T1(k - 1, 0), R2(k - 2), T1(k - 1, 1)
+                if k < NP:
+                    T2(k - 2, 0), T2(k - 2, 1)
         S2(NP - 1), E2(NP - 1), T2(NP - 2, 0), R2(NP - 1), T2(NP - 2, 1), T2(NP - 1, 0), T2(NP - 1, 1)

@@ -377,7 +377,7 @@ def tile_rlstmcell_pa_kernel(
                 op0=ALU.mult,
                 op1=ALU.add,
             )
-            if q == NP - 1:
+            if q >= NP - 2:
                 nc.sync.dma_start(out=out[:, 2 * q + i, :], in_=o[:, i, :])
             elif i == 1:
                 nc.sync.dma_start(out=out[:, 2 * q : 2 * q + 2, :], in_=o[:])

@@ -14,12 +14,14 @@ ALU = mybir.AluOpType
 P = 128
 S = 16
 D = 512
+PACK = 4
+PAIRS = S // 2
 EPS = 1e-9
-NP = S // 2
 FLOPS = 2 * 2 * (P * S) * D * D
 
-PINNED = True
-V_STATS = (0, 1)
+VECTOR_PAIRS = (0, 1)
+FIRST_FREE_CYCLE = 6
+BANKS_OF_Y2 = ("ys", "ys", "yn", "zt", "zt", "ys", "yn", "zt")
 
 
 def tile_rlstmcell_pa_kernel(
@@ -31,11 +33,21 @@ def tile_rlstmcell_pa_kernel(
         work = ctx.enter_context(tc.tile_pool(name="work", bufs=3))
         small = ctx.enter_context(tc.tile_pool(name="small", bufs=5))
         psum = ctx.enter_context(tc.psum_pool(name="psum", bufs=2))
-        if PINNED:
-            ctx.enter_context(tc.manual_schedule())
+        ctx.enter_context(tc.manual_schedule())
 
         def bank(tag, name):
             return psum.tile([P, D], F32, tag=tag, bufs=(4 if tag == "zt" else 2), name=name)
+
+        live = {}
+
+        def is_pair(q):
+            return 0 <= q < PAIRS
+
+        def on_scalar(q):
+            return is_pair(q) and q not in VECTOR_PAIRS
+
+        def on_vector(q):
+            return q in VECTOR_PAIRS
 
         rows1 = const.tile([P, P], BF16)
         nc.vector.memset(rows1[:], 0.0)
@@ -44,11 +56,13 @@ def tile_rlstmcell_pa_kernel(
         nc.vector.memset(warm_in[:], 1.0)
         ident = const.tile([P, P], F32)
         make_identity(nc, ident[:])
+        minus_one = const.tile([P, 2], F32)
+        nc.gpsimd.memset(minus_one[:], -1.0)
 
         nc.scalar.dma_start(out=rows1[0:4, :], in_=mlp_gain_1.rearrange("(j c) -> j c", c=P))
         nc.scalar.dma_start(out=rows1[4:8, :], in_=mlp_bias_1.rearrange("(j c) -> j c", c=P))
         nc.scalar.sqrt(out=warm_out[:], in_=warm_in[:])
-        w1raw = const.tile([P, 4, D], BF16)
+        w1raw = const.tile([P, PACK, D], BF16)
         nc.sync.dma_start(
             out=w1raw[:].rearrange("q (u e) c -> q u e c", u=2),
             in_=mlp_kernel_1.rearrange("(u q e) c -> q u e c", u=2, e=2),
@@ -56,33 +70,27 @@ def tile_rlstmcell_pa_kernel(
         x_all = const.tile([P, S, D], BF16)
         for lo, hi in ((0, 2), (2, 4), (4, 8), (8, 12), (12, 16)):
             nc.sync.dma_start(out=x_all[:, lo:hi, :], in_=c_att[:, lo:hi, :])
-        w2raw = const.tile([P, 4, D], BF16)
+        w2raw = const.tile([P, PACK, D], BF16)
         nc.sync.dma_start(out=w2raw[:], in_=mlp_kernel_2.rearrange("(j p) c -> p j c", p=P))
         gb2 = const.tile([P, 2, D], BF16)
         nc.sync.dma_start(out=gb2[:, 0, :], in_=mlp_gain_2.partition_broadcast(P))
         nc.sync.dma_start(out=gb2[:, 1, :], in_=mlp_bias_2.partition_broadcast(P))
         x_words = x_all[:].rearrange("p s d -> p (s d)").bitcast(F32)
 
-        live = {}
-
         rows1f = const.tile([P, P], F32)
+        nc.gpsimd.tensor_copy(out=rows1f[:], in_=rows1[:])
         gb1 = const.tile([P, 8], F32)
 
-        def gains1_cast():
-            nc.vector.tensor_copy(out=rows1f[:], in_=rows1[:])
-
-        def gains1_transpose():
-            live["gb1_ps"] = bank("yn", "gb1_ps")
-            nc.tensor.transpose(out=live["gb1_ps"][:, 0:P], in_=rows1f[:], identity=ident[:])
-
-        def gains1_copy():
-            nc.vector.tensor_copy(out=gb1[:], in_=live["gb1_ps"][:, 0:8])
+        def gains1_to_partitions():
+            gb1_ps = bank("yn", "gb1_ps")
+            nc.tensor.transpose(out=gb1_ps[:, 0:P], in_=rows1f[:], identity=ident[:])
+            nc.vector.tensor_copy(out=gb1[:], in_=gb1_ps[:, 0:8])
 
         wg = {}
         wcodes = {}
         wscales = {}
         for label in ("w1", "w2"):
-            wg[label] = const.tile([P, D, 4], BF16, align_bytes=64, name=label + "_grouped")
+            wg[label] = const.tile([P, D, PACK], BF16, align_bytes=64, name=label + "_grouped")
             wcodes[label] = const.tile([P, D], U32, align_bytes=64, name=label + "_codes")
             wscales[label] = const.tile([P, D], U8, align_bytes=64, name=label + "_scales")
         xcodes = const.tile([P, S * P], U32, align_bytes=64)
@@ -103,10 +111,7 @@ def tile_rlstmcell_pa_kernel(
                 in_=wg[label][:, lo:hi, :].rearrange("p c t -> p (c t)"),
             )
 
-        def ok(q):
-            return 0 <= q < NP
-
-        def mx(dst, codes, scales, s, label):
+        def matmul_tile(dst, codes, scales, s, label):
             nc.tensor.matmul_mx(
                 out=dst[:],
                 lhsT=codes[:, s * P : (s + 1) * P].bitcast(FP8X4),
@@ -117,8 +122,8 @@ def tile_rlstmcell_pa_kernel(
                 stop=True,
             )
 
-        def XT(q):
-            if not ok(q):
+        def x_transpose(q):
+            if not is_pair(q):
                 return
             xt = bank("zt", "xt")
             live["xt", q] = xt
@@ -131,8 +136,8 @@ def tile_rlstmcell_pa_kernel(
                         identity=ident[:],
                     )
 
-        def XC(q):
-            if not ok(q):
+        def x_copy(q):
+            if not is_pair(q):
                 return
             xg = work.tile([P, 2 * D], BF16, align_bytes=64, tag="xg", bufs=4, name="xg")
             live["xg", q] = xg
@@ -141,21 +146,11 @@ def tile_rlstmcell_pa_kernel(
                 in_=live["xt", q][:].rearrange("p (i u k) -> p i k u", i=2, u=2),
             )
 
-        def XQ(q):
-            if not ok(q):
+        def x_quantise(q):
+            if not is_pair(q):
                 return
             cols = slice(2 * q * P, (2 * q + 2) * P)
             nc.vector.quantize_mx(out=xcodes[:, cols].bitcast(FP8X4), scales=xscales[:, cols], in_=live["xg", q][:])
-
-        def MS(q, i):
-            if ok(q):
-                live["ys", q, i] = bank("ys", "ys")
-                mx(live["ys", q, i], xcodes, xscales, 2 * q + i, "w1")
-
-        def MN(q, i):
-            if ok(q):
-                live["yn", q, i] = bank("yn", "yn")
-                mx(live["yn", q, i], xcodes, xscales, 2 * q + i, "w1")
 
         def moments(key, q, i, src):
             if i == 0:
@@ -167,52 +162,50 @@ def tile_rlstmcell_pa_kernel(
                 live[key + "mv", q] = small.tile([P, 2, 2], F32, tag=key + "mv", name=key + "mv")
             nc.vector.bn_aggr(out=live[key + "mv", q][:, i, :], in_=live[key + "st", q][:, i, :])
 
-        def BN(q, i):
-            if ok(q):
-                moments("a", q, i, "ys")
-
-        def AG(q, i):
-            if ok(q):
-                aggregate("a", q, i)
-
-        def root(key, q, src_ap, divisor):
+        def inverse_deviation(key, q, sums, divisor):
             sd = small.tile([P, 2], F32, tag=key + "sd", name=key + "sd")
-            live[key + "sd", q] = sd
-            nc.scalar.activation(out=sd[:], in_=src_ap, func=ACT.Sqrt, scale=1.0 / divisor)
-
-        def add_eps(key, q):
+            nc.scalar.activation(out=sd[:], in_=sums, func=ACT.Sqrt, scale=1.0 / divisor)
             sde = small.tile([P, 2], F32, tag=key + "sde", name=key + "sde")
-            live[key + "sde", q] = sde
-            nc.vector.tensor_scalar_add(out=sde[:], in0=live[key + "sd", q][:], scalar1=EPS)
-
-        def invert(key, q):
+            nc.gpsimd.tensor_scalar(out=sde[:], in0=sd[:], scalar1=1.0, scalar2=EPS, op0=ALU.mult, op1=ALU.add)
             r = small.tile([P, 2], F32, tag=key + "r", name=key + "r")
             live[key + "r", q] = r
-            nc.vector.reciprocal(out=r[:], in_=live[key + "sde", q][:])
+            nc.gpsimd.tensor_tensor(out=r[:], in0=sde[:], in1=minus_one[:], op=ALU.pow)
 
-        def SQ(q):
-            if ok(q):
-                root("a", q, live["amv", q][:, :, 1], 1)
+        def mm1_for_statistics(q, i):
+            if is_pair(q):
+                live["ys", q, i] = bank("ys", "ys")
+                matmul_tile(live["ys", q, i], xcodes, xscales, 2 * q + i, "w1")
 
-        def E1(q):
-            if ok(q):
-                add_eps("a", q)
+        def mm1_to_normalise(q, i):
+            if is_pair(q):
+                live["yn", q, i] = bank("yn", "yn")
+                matmul_tile(live["yn", q, i], xcodes, xscales, 2 * q + i, "w1")
 
-        def R1(q):
-            if ok(q):
-                invert("a", q)
+        def ln1_moments(q, i):
+            if is_pair(q):
+                moments("a", q, i, "ys")
 
-        def N1(q):
-            if not ok(q):
+        def ln1_aggregate(q):
+            if not is_pair(q):
                 return
-            nmr = small.tile([P, 2], F32, tag="anmr", name="anmr")
-            live["anmr", q] = nmr
-            nc.vector.scalar_tensor_tensor(
-                out=nmr[:], in0=live["amv", q][:, :, 0], scalar=-1.0, in1=live["ar", q][:], op0=ALU.mult, op1=ALU.mult
+            aggregate("a", q, 0)
+            aggregate("a", q, 1)
+            nm = small.tile([P, 2], F32, tag="anm", name="anm")
+            live["anm", q] = nm
+            nc.gpsimd.tensor_scalar(
+                out=nm[:], in0=live["amv", q][:, :, 0], scalar1=-1.0, scalar2=0.0, op0=ALU.mult, op1=ALU.add
             )
 
-        def NR(q, i):
-            if not ok(q):
+        def ln1_scalars(q):
+            if not is_pair(q):
+                return
+            inverse_deviation("a", q, live["amv", q][:, :, 1], 1)
+            nmr = small.tile([P, 2], F32, tag="anmr", name="anmr")
+            live["anmr", q] = nmr
+            nc.gpsimd.tensor_tensor(out=nmr[:], in0=live["anm", q][:], in1=live["ar", q][:], op=ALU.mult)
+
+        def ln1_normalise(q, i):
+            if not is_pair(q):
                 return
             if i == 0:
                 live["z", q] = work.tile([P, 2, D], F32, tag="z", name="z")
@@ -224,13 +217,13 @@ def tile_rlstmcell_pa_kernel(
                 scale=live["ar", q][:, i : i + 1],
             )
 
-        def ZT(q):
-            if not ok(q):
+        def z_transpose(q):
+            if not is_pair(q):
                 return
             zts = [bank("zt", "zt"), bank("zt", "zt")]
             live["zt", q] = zts
             for i in range(2):
-                for j in range(4):
+                for j in range(PACK):
                     col = (2 * (j % 2) + i) * P
                     nc.tensor.transpose(
                         out=zts[j // 2][:, col : col + P],
@@ -238,32 +231,32 @@ def tile_rlstmcell_pa_kernel(
                         identity=ident[:],
                     )
 
-        def RL(q, js):
-            if not ok(q):
+        def h_activate(q, blocks):
+            if not is_pair(q):
                 return
-            if js[0] == 0:
-                live["hp", q] = work.tile([P, 4, 2 * P], BF16, tag="hp", name="hp")
-            for j in js:
+            if blocks[0] == 0:
+                live["hp", q] = work.tile([P, PACK, 2 * P], BF16, tag="hp", name="hp")
+            for j in blocks:
                 nc.scalar.activation(
                     out=live["hp", q][:, j, :],
                     in_=live["zt", q][j // 2][:, (j % 2) * 2 * P : (j % 2 + 1) * 2 * P],
                     func=ACT.Relu,
-                    bias=gb1[:, 4 + j : 5 + j],
+                    bias=gb1[:, PACK + j : PACK + j + 1],
                     scale=gb1[:, j : j + 1],
                 )
 
-        def RG(q):
-            if not ok(q):
+        def h_regroup(q):
+            if not is_pair(q):
                 return
-            hg = work.tile([P, 2 * P, 4], BF16, align_bytes=64, tag="hg", name="hg")
+            hg = work.tile([P, 2 * P, PACK], BF16, align_bytes=64, tag="hg", name="hg")
             live["hg", q] = hg
             nc.vector.tensor_copy(
                 out=hg[:].rearrange("p (c i) t -> p c t i", i=4),
                 in_=live["hp", q][:].rearrange("p t (c i) -> p c t i", i=4),
             )
 
-        def HQ(q):
-            if not ok(q):
+        def h_quantise(q):
+            if not is_pair(q):
                 return
             cols = slice(2 * q * P, (2 * q + 2) * P)
             nc.vector.quantize_mx(
@@ -272,16 +265,15 @@ def tile_rlstmcell_pa_kernel(
                 in_=live["hg", q][:].rearrange("p k t -> p (k t)"),
             )
 
-        def M2(q):
-            if not ok(q):
+        def mm2(q):
+            if not is_pair(q):
                 return
-            tag = ("ys", "ys", "yn", "zt", "zt", "ys", "yn", "zt")[q]
             for i in range(2):
-                live["y2", q, i] = bank(tag, "y2")
-                mx(live["y2", q, i], hcodes, hscales, 2 * q + i, "w2")
+                live["y2", q, i] = bank(BANKS_OF_Y2[q], "y2")
+                matmul_tile(live["y2", q, i], hcodes, hscales, 2 * q + i, "w2")
 
-        def PA(q, i):
-            if not ok(q) or q in V_STATS:
+        def ln2_copy_and_sum(q, i):
+            if not on_scalar(q):
                 return
             if i == 0:
                 live["y2s", q] = work.tile([P, 2, D], F32, tag="y2s", name="y2s")
@@ -293,15 +285,15 @@ def tile_rlstmcell_pa_kernel(
                 accum_out=live["tot", q][:, i : i + 1],
             )
 
-        def MU(q):
-            if not ok(q) or q in V_STATS:
+        def ln2_minus_mean(q):
+            if not on_scalar(q):
                 return
             negmu = small.tile([P, 2], F32, tag="negmu", name="negmu")
             live["negmu", q] = negmu
             nc.scalar.mul(out=negmu[:], in_=live["tot", q][:], mul=-1.0 / D)
 
-        def PB(q):
-            if not ok(q) or q in V_STATS:
+        def ln2_squared_deviations(q):
+            if not on_scalar(q):
                 return
             ssq = small.tile([P, 2], F32, tag="ssq", name="ssq")
             live["ssq", q] = ssq
@@ -315,36 +307,16 @@ def tile_rlstmcell_pa_kernel(
                     accum_out=ssq[:, i : i + 1],
                 )
 
-        def B2(q, i):
-            if ok(q) and q in V_STATS:
-                moments("b", q, i, "y2")
+        def ln2_scalars(q):
+            if on_vector(q):
+                inverse_deviation("b", q, live["bmv", q][:, :, 1], 1)
+            elif on_scalar(q):
+                inverse_deviation("b", q, live["ssq", q][:], D)
 
-        def A2(q, i):
-            if ok(q) and q in V_STATS:
-                aggregate("b", q, i)
-
-        def S2(q):
-            if not ok(q):
-                return
-            if q in V_STATS:
-                root("b", q, live["bmv", q][:, :, 1], 1)
-            else:
-                root("b", q, live["ssq", q][:], D)
-
-        def E2(q):
-            if ok(q):
-                add_eps("b", q)
-
-        def R2(q):
-            if ok(q):
-                invert("b", q)
-
-        def T1(q, i):
-            if not ok(q):
-                return
+        def ln2_centre_and_gain(q, i):
             if i == 0:
                 live["t", q] = work.tile([P, 2, D], F32, tag="t", name="t")
-            if q in V_STATS:
+            if on_vector(q):
                 nc.vector.scalar_tensor_tensor(
                     out=live["t", q][:, i, :],
                     in0=live["y2", q, i][:],
@@ -363,98 +335,82 @@ def tile_rlstmcell_pa_kernel(
                     op1=ALU.mult,
                 )
 
-        def T2(q, i):
-            if not ok(q):
+        def ln2_scale_bias_store(q):
+            if not is_pair(q):
                 return
-            if i == 0:
-                live["o", q] = work.tile([P, 2, D], F32, tag="o", bufs=4, name="o")
-            o = live["o", q]
-            nc.vector.scalar_tensor_tensor(
-                out=o[:, i, :],
-                in0=live["t", q][:, i, :],
-                scalar=live["br", q][:, i : i + 1],
-                in1=gb2[:, 1, :],
-                op0=ALU.mult,
-                op1=ALU.add,
-            )
-            if q >= NP - 2:
-                nc.sync.dma_start(out=out[:, 2 * q + i, :], in_=o[:, i, :])
-            elif i == 1:
+            o = work.tile([P, 2, D], F32, tag="o", bufs=4, name="o")
+            for i in range(2):
+                nc.vector.scalar_tensor_tensor(
+                    out=o[:, i, :],
+                    in0=live["t", q][:, i, :],
+                    scalar=live["br", q][:, i : i + 1],
+                    in1=gb2[:, 1, :],
+                    op0=ALU.mult,
+                    op1=ALU.add,
+                )
+                if q >= PAIRS - 2:
+                    nc.sync.dma_start(out=out[:, 2 * q + i, :], in_=o[:, i, :])
+            if q < PAIRS - 2:
                 nc.sync.dma_start(out=out[:, 2 * q : 2 * q + 2, :], in_=o[:])
 
-        def late(n, i):
-            u = n - 6
-            if 0 <= u <= 3:
-                if u % 2 == 0:
-                    B2(u // 2, i)
-                else:
-                    T1(u // 2, i)
+        def vector_pair_pass(n, i):
+            for v in VECTOR_PAIRS:
+                if n == FIRST_FREE_CYCLE + 2 * v:
+                    moments("b", v, i, "y2")
+                if n == FIRST_FREE_CYCLE + 2 * v + 1:
+                    ln2_centre_and_gain(v, i)
 
         regroup_weight("w1", w1raw, 0, 256)
         regroup_weight("w1", w1raw, 256, 512)
         quantise_weight("w1", 0, 256)
         quantise_weight("w1", 256, 512)
-        XT(0), XC(0), XT(1), XC(1), XQ(0), XT(2), XC(2), XT(3), XC(3), MS(0, 0), MS(0, 1), XQ(1)
-        XT(4), XC(4), XT(5), XC(5)
-        BN(0, 0), BN(0, 1), gains1_cast(), MS(1, 0), MS(1, 1), XT(6), XT(7), gains1_transpose()
-        XQ(2), AG(0, 0), XQ(3), AG(0, 1), SQ(0), XC(6)
-        BN(1, 0), E1(0), gains1_copy(), MN(0, 0), MN(0, 1), BN(1, 1), MS(2, 0), MS(2, 1)
-        R1(0), AG(1, 0), XQ(4), AG(1, 1), N1(0), XC(7), SQ(1)
-        BN(2, 0), BN(2, 1), MS(3, 0), MS(3, 1), E1(1), AG(2, 0)
-        regroup_weight("w2", w2raw, 0, 128)
-        R1(1), AG(2, 1)
-        regroup_weight("w2", w2raw, 128, 256)
-        N1(1)
-        NR(0, 0), NR(0, 1), SQ(2), MN(1, 0), MN(1, 1), ZT(0)
-        for n in range(1, NP + 3):
-            NR(n, 0), NR(n, 1)
-            BN(n + 2, 0), late(n, 0), MS(n + 3, 0), MN(n + 1, 0), MN(n + 1, 1), E1(n + 1)
-            if n == 8:
-                E2(0)
-            BN(n + 2, 1), late(n, 1), MS(n + 3, 1)
-            if n == 5:
-                M2(0)
-            if n == 7:
-                M2(1)
-            ZT(n), R1(n + 1)
-            if n == 8:
-                R2(0)
-            RG(n - 2)
-            if n == 1:
-                regroup_weight("w2", w2raw, 256, 384)
-            AG(n + 2, 0), AG(n + 2, 1)
-            if n == 6 or n == 8:
-                A2((n - 6) // 2, 0), A2((n - 6) // 2, 1)
-            N1(n + 1), HQ(n - 3)
-            if n <= 3:
-                XQ(n + 4)
-            if n == 2:
-                regroup_weight("w2", w2raw, 384, 512)
-            if n == 3:
-                quantise_weight("w2", 0, 256)
-            if n == 4:
-                quantise_weight("w2", 256, 512)
-            if n == 9:
-                T2(0, 0), T2(0, 1)
-            RL(n - 1, (0, 1, 2, 3)), SQ(n + 2)
-            if n == 7:
-                S2(0), M2(2)
-            if n == 8:
-                M2(3), M2(4)
-            if n == 9:
-                M2(5)
-        for k in range(2, NP + 1):
-            PA(k, 0)
-            if k == 3:
-                MU(2)
-            if k >= 3:
-                S2(k - 2)
-            PA(k, 1)
-            if k <= 3:
-                M2(k + 4)
-            if k >= 3:
-                PB(k - 1), MU(k)
-                E2(k - 2), T1(k - 1, 0), R2(k - 2), T1(k - 1, 1)
-                if k < NP:
-                    T2(k - 2, 0), T2(k - 2, 1)
-        S2(NP - 1), E2(NP - 1), T2(NP - 2, 0), R2(NP - 1), T2(NP - 2, 1), T2(NP - 1, 0), T2(NP - 1, 1)
+
+        for n in range(-7, PAIRS + 3):
+            x_transpose(n + 7)
+            if n == -1:
+                gains1_to_partitions()
+            ln1_normalise(n, 0)
+            ln1_normalise(n, 1)
+            ln1_moments(n + 2, 0)
+            vector_pair_pass(n, 0)
+            mm1_for_statistics(n + 3, 0)
+            mm1_to_normalise(n + 1, 0)
+            mm1_to_normalise(n + 1, 1)
+            ln1_moments(n + 2, 1)
+            vector_pair_pass(n, 1)
+            mm1_for_statistics(n + 3, 1)
+            for v in VECTOR_PAIRS:
+                if n == FIRST_FREE_CYCLE + 2 * v - 1:
+                    mm2(v)
+            z_transpose(n)
+            x_copy(n + 7)
+            h_regroup(n - 2)
+            ln1_aggregate(n + 2)
+            for v in VECTOR_PAIRS:
+                if n == FIRST_FREE_CYCLE + 2 * v:
+                    aggregate("b", v, 0)
+                    aggregate("b", v, 1)
+            h_quantise(n - 3)
+            x_quantise(n + 4)
+            if -1 <= n < 3:
+                regroup_weight("w2", w2raw, 128 * (n + 1), 128 * (n + 2))
+            if 3 <= n < 5:
+                quantise_weight("w2", 256 * (n - 3), 256 * (n - 2))
+            h_activate(n - 1, (0, 1, 2))
+            ln1_scalars(n + 2)
+            h_activate(n - 1, (3,))
+
+        first = len(VECTOR_PAIRS)
+        mm2(first)
+        mm2(first + 1)
+        for k in range(first, PAIRS + 2):
+            mm2(k + 2)
+            ln2_copy_and_sum(k, 0)
+            ln2_minus_mean(k - 1)
+            ln2_scalars(k - 2)
+            ln2_copy_and_sum(k, 1)
+            ln2_squared_deviations(k - 1)
+            if on_scalar(k - 1):
+                ln2_centre_and_gain(k - 1, 0)
+                ln2_centre_and_gain(k - 1, 1)
+            ln2_scale_bias_store(k - 2)

@@ -43,11 +43,11 @@ def tile_rlstmcell_pa_kernel(
         def is_pair(q):
             return 0 <= q < PAIRS
 
-        def on_scalar(q):
-            return is_pair(q) and q not in VECTOR_PAIRS
-
         def on_vector(q):
             return q in VECTOR_PAIRS
+
+        def on_scalar(q):
+            return is_pair(q) and not on_vector(q)
 
         rows1 = const.tile([P, P], BF16)
         nc.vector.memset(rows1[:], 0.0)
@@ -56,8 +56,6 @@ def tile_rlstmcell_pa_kernel(
         nc.vector.memset(warm_in[:], 1.0)
         ident = const.tile([P, P], F32)
         make_identity(nc, ident[:])
-        minus_one = const.tile([P, 2], F32)
-        nc.gpsimd.memset(minus_one[:], -1.0)
 
         nc.scalar.dma_start(out=rows1[0:4, :], in_=mlp_gain_1.rearrange("(j c) -> j c", c=P))
         nc.scalar.dma_start(out=rows1[4:8, :], in_=mlp_bias_1.rearrange("(j c) -> j c", c=P))
@@ -75,16 +73,16 @@ def tile_rlstmcell_pa_kernel(
         gb2 = const.tile([P, 2, D], BF16)
         nc.sync.dma_start(out=gb2[:, 0, :], in_=mlp_gain_2.partition_broadcast(P))
         nc.sync.dma_start(out=gb2[:, 1, :], in_=mlp_bias_2.partition_broadcast(P))
-        x_words = x_all[:].rearrange("p s d -> p (s d)").bitcast(F32)
+        x_as_f32 = x_all[:].rearrange("p s d -> p (s d)").bitcast(F32)
 
         rows1f = const.tile([P, P], F32)
         nc.gpsimd.tensor_copy(out=rows1f[:], in_=rows1[:])
-        gb1 = const.tile([P, 8], F32)
+        gb1 = const.tile([P, 2 * PACK], F32)
 
         def gains1_to_partitions():
             gb1_ps = bank("yn", "gb1_ps")
             nc.tensor.transpose(out=gb1_ps[:, 0:P], in_=rows1f[:], identity=ident[:])
-            nc.vector.tensor_copy(out=gb1[:], in_=gb1_ps[:, 0:8])
+            nc.vector.tensor_copy(out=gb1[:], in_=gb1_ps[:, 0 : 2 * PACK])
 
         wg = {}
         wcodes = {}
@@ -111,7 +109,7 @@ def tile_rlstmcell_pa_kernel(
                 in_=wg[label][:, lo:hi, :].rearrange("p c t -> p (c t)"),
             )
 
-        def matmul_tile(dst, codes, scales, s, label):
+        def matmul_slot(dst, codes, scales, s, label):
             nc.tensor.matmul_mx(
                 out=dst[:],
                 lhsT=codes[:, s * P : (s + 1) * P].bitcast(FP8X4),
@@ -129,10 +127,10 @@ def tile_rlstmcell_pa_kernel(
             live["xt", q] = xt
             for i in range(2):
                 for u in range(2):
-                    col = (2 * q + i) * 256 + u * P
+                    col = (2 * q + i) * (D // 2) + u * P
                     nc.tensor.transpose(
                         out=xt[:, (2 * i + u) * P : (2 * i + u + 1) * P],
-                        in_=x_words[:, col : col + P],
+                        in_=x_as_f32[:, col : col + P],
                         identity=ident[:],
                     )
 
@@ -157,52 +155,60 @@ def tile_rlstmcell_pa_kernel(
                 live[key + "st", q] = small.tile([P, 2, 6], F32, tag=key + "st", name=key + "st")
             nc.vector.bn_stats(out=live[key + "st", q][:, i, :], in_=live[src, q, i][:])
 
-        def aggregate(key, q, i):
-            if i == 0:
-                live[key + "mv", q] = small.tile([P, 2, 2], F32, tag=key + "mv", name=key + "mv")
-            nc.vector.bn_aggr(out=live[key + "mv", q][:, i, :], in_=live[key + "st", q][:, i, :])
+        def aggregate(key, q):
+            live[key + "mv", q] = small.tile([P, 2, 2], F32, tag=key + "mv", name=key + "mv")
+            for i in range(2):
+                nc.vector.bn_aggr(out=live[key + "mv", q][:, i, :], in_=live[key + "st", q][:, i, :])
 
-        def inverse_deviation(key, q, sums, divisor):
+        def root(key, q, sums, divisor):
             sd = small.tile([P, 2], F32, tag=key + "sd", name=key + "sd")
+            live[key + "sd", q] = sd
             nc.scalar.activation(out=sd[:], in_=sums, func=ACT.Sqrt, scale=1.0 / divisor)
+
+        def add_eps(key, q):
+            if not is_pair(q):
+                return
             sde = small.tile([P, 2], F32, tag=key + "sde", name=key + "sde")
-            nc.gpsimd.tensor_scalar(out=sde[:], in0=sd[:], scalar1=1.0, scalar2=EPS, op0=ALU.mult, op1=ALU.add)
+            live[key + "sde", q] = sde
+            nc.vector.tensor_scalar_add(out=sde[:], in0=live[key + "sd", q][:], scalar1=EPS)
+
+        def invert(key, q):
+            if not is_pair(q):
+                return
             r = small.tile([P, 2], F32, tag=key + "r", name=key + "r")
             live[key + "r", q] = r
-            nc.gpsimd.tensor_tensor(out=r[:], in0=sde[:], in1=minus_one[:], op=ALU.pow)
+            nc.vector.reciprocal(out=r[:], in_=live[key + "sde", q][:])
 
         def mm1_for_statistics(q, i):
             if is_pair(q):
                 live["ys", q, i] = bank("ys", "ys")
-                matmul_tile(live["ys", q, i], xcodes, xscales, 2 * q + i, "w1")
+                matmul_slot(live["ys", q, i], xcodes, xscales, 2 * q + i, "w1")
 
         def mm1_to_normalise(q, i):
             if is_pair(q):
                 live["yn", q, i] = bank("yn", "yn")
-                matmul_tile(live["yn", q, i], xcodes, xscales, 2 * q + i, "w1")
+                matmul_slot(live["yn", q, i], xcodes, xscales, 2 * q + i, "w1")
 
         def ln1_moments(q, i):
             if is_pair(q):
                 moments("a", q, i, "ys")
 
         def ln1_aggregate(q):
-            if not is_pair(q):
-                return
-            aggregate("a", q, 0)
-            aggregate("a", q, 1)
-            nm = small.tile([P, 2], F32, tag="anm", name="anm")
-            live["anm", q] = nm
-            nc.gpsimd.tensor_scalar(
-                out=nm[:], in0=live["amv", q][:, :, 0], scalar1=-1.0, scalar2=0.0, op0=ALU.mult, op1=ALU.add
-            )
+            if is_pair(q):
+                aggregate("a", q)
 
-        def ln1_scalars(q):
+        def ln1_root(q):
+            if is_pair(q):
+                root("a", q, live["amv", q][:, :, 1], 1)
+
+        def ln1_shift(q):
             if not is_pair(q):
                 return
-            inverse_deviation("a", q, live["amv", q][:, :, 1], 1)
             nmr = small.tile([P, 2], F32, tag="anmr", name="anmr")
             live["anmr", q] = nmr
-            nc.gpsimd.tensor_tensor(out=nmr[:], in0=live["anm", q][:], in1=live["ar", q][:], op=ALU.mult)
+            nc.vector.scalar_tensor_tensor(
+                out=nmr[:], in0=live["amv", q][:, :, 0], scalar=-1.0, in1=live["ar", q][:], op0=ALU.mult, op1=ALU.mult
+            )
 
         def ln1_normalise(q, i):
             if not is_pair(q):
@@ -231,12 +237,11 @@ def tile_rlstmcell_pa_kernel(
                         identity=ident[:],
                     )
 
-        def h_activate(q, blocks):
+        def h_activate(q):
             if not is_pair(q):
                 return
-            if blocks[0] == 0:
-                live["hp", q] = work.tile([P, PACK, 2 * P], BF16, tag="hp", name="hp")
-            for j in blocks:
+            live["hp", q] = work.tile([P, PACK, 2 * P], BF16, tag="hp", name="hp")
+            for j in range(PACK):
                 nc.scalar.activation(
                     out=live["hp", q][:, j, :],
                     in_=live["zt", q][j // 2][:, (j % 2) * 2 * P : (j % 2 + 1) * 2 * P],
@@ -270,7 +275,7 @@ def tile_rlstmcell_pa_kernel(
                 return
             for i in range(2):
                 live["y2", q, i] = bank(BANKS_OF_Y2[q], "y2")
-                matmul_tile(live["y2", q, i], hcodes, hscales, 2 * q + i, "w2")
+                matmul_slot(live["y2", q, i], hcodes, hscales, 2 * q + i, "w2")
 
         def ln2_copy_and_sum(q, i):
             if not on_scalar(q):
@@ -307,11 +312,11 @@ def tile_rlstmcell_pa_kernel(
                     accum_out=ssq[:, i : i + 1],
                 )
 
-        def ln2_scalars(q):
+        def ln2_root(q):
             if on_vector(q):
-                inverse_deviation("b", q, live["bmv", q][:, :, 1], 1)
+                root("b", q, live["bmv", q][:, :, 1], 1)
             elif on_scalar(q):
-                inverse_deviation("b", q, live["ssq", q][:], D)
+                root("b", q, live["ssq", q][:], D)
 
         def ln2_centre_and_gain(q, i):
             if i == 0:
@@ -335,25 +340,26 @@ def tile_rlstmcell_pa_kernel(
                     op1=ALU.mult,
                 )
 
-        def ln2_scale_bias_store(q):
+        def ln2_scale_bias_store(q, i):
             if not is_pair(q):
                 return
-            o = work.tile([P, 2, D], F32, tag="o", bufs=4, name="o")
-            for i in range(2):
-                nc.vector.scalar_tensor_tensor(
-                    out=o[:, i, :],
-                    in0=live["t", q][:, i, :],
-                    scalar=live["br", q][:, i : i + 1],
-                    in1=gb2[:, 1, :],
-                    op0=ALU.mult,
-                    op1=ALU.add,
-                )
-                if q >= PAIRS - 2:
-                    nc.sync.dma_start(out=out[:, 2 * q + i, :], in_=o[:, i, :])
-            if q < PAIRS - 2:
+            if i == 0:
+                live["o", q] = work.tile([P, 2, D], F32, tag="o", bufs=4, name="o")
+            o = live["o", q]
+            nc.vector.scalar_tensor_tensor(
+                out=o[:, i, :],
+                in0=live["t", q][:, i, :],
+                scalar=live["br", q][:, i : i + 1],
+                in1=gb2[:, 1, :],
+                op0=ALU.mult,
+                op1=ALU.add,
+            )
+            if q >= PAIRS - 2:
+                nc.sync.dma_start(out=out[:, 2 * q + i, :], in_=o[:, i, :])
+            elif i == 1:
                 nc.sync.dma_start(out=out[:, 2 * q : 2 * q + 2, :], in_=o[:])
 
-        def vector_pair_pass(n, i):
+        def vector_pair_step(n, i):
             for v in VECTOR_PAIRS:
                 if n == FIRST_FREE_CYCLE + 2 * v:
                     moments("b", v, i, "y2")
@@ -372,45 +378,49 @@ def tile_rlstmcell_pa_kernel(
             ln1_normalise(n, 0)
             ln1_normalise(n, 1)
             ln1_moments(n + 2, 0)
-            vector_pair_pass(n, 0)
+            vector_pair_step(n, 0)
             mm1_for_statistics(n + 3, 0)
             mm1_to_normalise(n + 1, 0)
             mm1_to_normalise(n + 1, 1)
+            add_eps("a", n + 1)
             ln1_moments(n + 2, 1)
-            vector_pair_pass(n, 1)
+            vector_pair_step(n, 1)
             mm1_for_statistics(n + 3, 1)
             for v in VECTOR_PAIRS:
                 if n == FIRST_FREE_CYCLE + 2 * v - 1:
                     mm2(v)
             z_transpose(n)
+            invert("a", n + 1)
             x_copy(n + 7)
             h_regroup(n - 2)
             ln1_aggregate(n + 2)
             for v in VECTOR_PAIRS:
                 if n == FIRST_FREE_CYCLE + 2 * v:
-                    aggregate("b", v, 0)
-                    aggregate("b", v, 1)
+                    aggregate("b", v)
+            ln1_shift(n + 1)
             h_quantise(n - 3)
             x_quantise(n + 4)
             if -1 <= n < 3:
                 regroup_weight("w2", w2raw, 128 * (n + 1), 128 * (n + 2))
             if 3 <= n < 5:
                 quantise_weight("w2", 256 * (n - 3), 256 * (n - 2))
-            h_activate(n - 1, (0, 1, 2))
-            ln1_scalars(n + 2)
-            h_activate(n - 1, (3,))
+            h_activate(n - 1)
+            ln1_root(n + 2)
 
         first = len(VECTOR_PAIRS)
         mm2(first)
         mm2(first + 1)
-        for k in range(first, PAIRS + 2):
+        for k in range(first, PAIRS + 3):
             mm2(k + 2)
             ln2_copy_and_sum(k, 0)
             ln2_minus_mean(k - 1)
-            ln2_scalars(k - 2)
+            ln2_root(k - 2)
             ln2_copy_and_sum(k, 1)
             ln2_squared_deviations(k - 1)
+            add_eps("b", k - 2)
+            ln2_scale_bias_store(k - 3, 0)
+            invert("b", k - 2)
+            ln2_scale_bias_store(k - 3, 1)
             if on_scalar(k - 1):
                 ln2_centre_and_gain(k - 1, 0)
                 ln2_centre_and_gain(k - 1, 1)
-            ln2_scale_bias_store(k - 2)

@@ -49,6 +49,13 @@ def tile_rlstmcell_pa_kernel(
         def on_scalar(q):
             return is_pair(q) and not on_vector(q)
 
+        def scalar_pair(q):
+            return q if on_scalar(q) else -1
+
+        def vector_pair_started_in(cycle):
+            v, odd = divmod(cycle - FIRST_FREE_CYCLE, 2)
+            return v if odd == 0 and on_vector(v) else -1
+
         rows1 = const.tile([P, P], BF16)
         nc.vector.memset(rows1[:], 0.0)
         warm_in = const.tile([P, 1], F32)
@@ -66,8 +73,8 @@ def tile_rlstmcell_pa_kernel(
             in_=mlp_kernel_1.rearrange("(u q e) c -> q u e c", u=2, e=2),
         )
         x_all = const.tile([P, S, D], BF16)
-        for lo, hi in ((0, 2), (2, 4), (4, 8), (8, 12), (12, 16)):
-            nc.sync.dma_start(out=x_all[:, lo:hi, :], in_=c_att[:, lo:hi, :])
+        for q in range(PAIRS):
+            nc.sync.dma_start(out=x_all[:, 2 * q : 2 * q + 2, :], in_=c_att[:, 2 * q : 2 * q + 2, :])
         w2raw = const.tile([P, PACK, D], BF16)
         nc.sync.dma_start(out=w2raw[:], in_=mlp_kernel_2.rearrange("(j p) c -> p j c", p=P))
         gb2 = const.tile([P, 2, D], BF16)
@@ -312,6 +319,14 @@ def tile_rlstmcell_pa_kernel(
                     accum_out=ssq[:, i : i + 1],
                 )
 
+        def ln2_moments(q, i):
+            if is_pair(q):
+                moments("b", q, i, "y2")
+
+        def ln2_aggregate(q):
+            if is_pair(q):
+                aggregate("b", q)
+
         def ln2_root(q):
             if on_vector(q):
                 root("b", q, live["bmv", q][:, :, 1], 1)
@@ -319,6 +334,8 @@ def tile_rlstmcell_pa_kernel(
                 root("b", q, live["ssq", q][:], D)
 
         def ln2_centre_and_gain(q, i):
+            if not is_pair(q):
+                return
             if i == 0:
                 live["t", q] = work.tile([P, 2, D], F32, tag="t", name="t")
             if on_vector(q):
@@ -359,68 +376,65 @@ def tile_rlstmcell_pa_kernel(
             elif i == 1:
                 nc.sync.dma_start(out=out[:, 2 * q : 2 * q + 2, :], in_=o[:])
 
-        def vector_pair_step(n, i):
-            for v in VECTOR_PAIRS:
-                if n == FIRST_FREE_CYCLE + 2 * v:
-                    moments("b", v, i, "y2")
-                if n == FIRST_FREE_CYCLE + 2 * v + 1:
-                    ln2_centre_and_gain(v, i)
-
         regroup_weight("w1", w1raw, 0, 256)
         regroup_weight("w1", w1raw, 256, 512)
         quantise_weight("w1", 0, 256)
         quantise_weight("w1", 256, 512)
 
-        for n in range(-7, PAIRS + 3):
+        for n in range(-7, PAIRS + 4):
+            starting = vector_pair_started_in(n)
+            started = vector_pair_started_in(n - 1)
             x_transpose(n + 7)
             if n == -1:
                 gains1_to_partitions()
             ln1_normalise(n, 0)
             ln1_normalise(n, 1)
             ln1_moments(n + 2, 0)
-            vector_pair_step(n, 0)
+            ln2_moments(starting, 0)
+            ln2_centre_and_gain(started, 0)
             mm1_for_statistics(n + 3, 0)
             mm1_to_normalise(n + 1, 0)
             mm1_to_normalise(n + 1, 1)
             add_eps("a", n + 1)
+            add_eps("b", started)
             ln1_moments(n + 2, 1)
-            vector_pair_step(n, 1)
+            ln2_moments(starting, 1)
+            ln2_centre_and_gain(started, 1)
             mm1_for_statistics(n + 3, 1)
-            for v in VECTOR_PAIRS:
-                if n == FIRST_FREE_CYCLE + 2 * v - 1:
-                    mm2(v)
+            mm2(vector_pair_started_in(n + 1))
             z_transpose(n)
             invert("a", n + 1)
+            invert("b", started)
             x_copy(n + 7)
             h_regroup(n - 2)
             ln1_aggregate(n + 2)
-            for v in VECTOR_PAIRS:
-                if n == FIRST_FREE_CYCLE + 2 * v:
-                    aggregate("b", v)
+            ln2_aggregate(starting)
             ln1_shift(n + 1)
             h_quantise(n - 3)
             x_quantise(n + 4)
+            ln2_scale_bias_store(vector_pair_started_in(n - 3), 0)
+            ln2_scale_bias_store(vector_pair_started_in(n - 3), 1)
             if -1 <= n < 3:
                 regroup_weight("w2", w2raw, 128 * (n + 1), 128 * (n + 2))
             if 3 <= n < 5:
                 quantise_weight("w2", 256 * (n - 3), 256 * (n - 2))
             h_activate(n - 1)
             ln1_root(n + 2)
+            ln2_root(starting)
 
         first = len(VECTOR_PAIRS)
         mm2(first)
         mm2(first + 1)
-        for k in range(first, PAIRS + 3):
+        for k in range(first, PAIRS + 2):
             mm2(k + 2)
             ln2_copy_and_sum(k, 0)
             ln2_minus_mean(k - 1)
-            ln2_root(k - 2)
+            ln2_root(scalar_pair(k - 2))
             ln2_copy_and_sum(k, 1)
             ln2_squared_deviations(k - 1)
-            add_eps("b", k - 2)
-            ln2_scale_bias_store(k - 3, 0)
-            invert("b", k - 2)
-            ln2_scale_bias_store(k - 3, 1)
-            if on_scalar(k - 1):
-                ln2_centre_and_gain(k - 1, 0)
-                ln2_centre_and_gain(k - 1, 1)
+            add_eps("b", scalar_pair(k - 2))
+            ln2_centre_and_gain(scalar_pair(k - 1), 0)
+            invert("b", scalar_pair(k - 2))
+            ln2_centre_and_gain(scalar_pair(k - 1), 1)
+            ln2_scale_bias_store(scalar_pair(k - 2), 0)
+            ln2_scale_bias_store(scalar_pair(k - 2), 1)

from contextlib import ExitStack

import concourse.mybir as mybir
from concourse.masks import make_identity

F32 = mybir.dt.float32
BF16 = mybir.dt.bfloat16
U32 = mybir.dt.uint32
U8 = mybir.dt.uint8
FP8X4 = mybir.dt.float8_e4m3fn_x4
ACT = mybir.ActivationFunctionType
ALU = mybir.AluOpType

P = 128
S = 16
D = 512
PACK = 4
PAIRS = S // 2
EPS = 1e-9
FLOPS = 2 * 2 * (P * S) * D * D

VECTOR_PAIRS = (0, 1)
FIRST_FREE_CYCLE = 6
BANKS_OF_Y2 = ("ys", "ys", "yn", "zt", "zt", "ys", "yn", "zt")


def tile_rlstmcell_pa_kernel(
    tc, c_att, mlp_kernel_1, mlp_kernel_2, mlp_gain_1, mlp_gain_2, mlp_bias_1, mlp_bias_2, out
):
    nc = tc.nc
    with ExitStack() as ctx:
        const = ctx.enter_context(tc.tile_pool(name="const", bufs=1))
        work = ctx.enter_context(tc.tile_pool(name="work", bufs=3))
        small = ctx.enter_context(tc.tile_pool(name="small", bufs=5))
        psum = ctx.enter_context(tc.psum_pool(name="psum", bufs=2))
        ctx.enter_context(tc.manual_schedule())

        def bank(tag, name):
            return psum.tile([P, D], F32, tag=tag, bufs=(4 if tag == "zt" else 2), name=name)

        live = {}

        def is_pair(q):
            return 0 <= q < PAIRS

        def on_vector(q):
            return q in VECTOR_PAIRS

        def on_scalar(q):
            return is_pair(q) and not on_vector(q)

        def scalar_pair(q):
            return q if on_scalar(q) else -1

        def vector_pair_started_in(cycle):
            v, odd = divmod(cycle - FIRST_FREE_CYCLE, 2)
            return v if odd == 0 and on_vector(v) else -1

        rows1 = const.tile([P, P], BF16)
        nc.vector.memset(rows1[:], 0.0)
        warm_in = const.tile([P, 1], F32)
        warm_out = const.tile([P, 1], F32)
        nc.vector.memset(warm_in[:], 1.0)
        ident = const.tile([P, P], F32)
        make_identity(nc, ident[:])

        nc.scalar.dma_start(out=rows1[0:4, :], in_=mlp_gain_1.rearrange("(j c) -> j c", c=P))
        nc.scalar.dma_start(out=rows1[4:8, :], in_=mlp_bias_1.rearrange("(j c) -> j c", c=P))
        nc.scalar.sqrt(out=warm_out[:], in_=warm_in[:])
        w1raw = const.tile([P, PACK, D], BF16)
        nc.sync.dma_start(
            out=w1raw[:].rearrange("q (u e) c -> q u e c", u=2),
            in_=mlp_kernel_1.rearrange("(u q e) c -> q u e c", u=2, e=2),
        )
        x_all = const.tile([P, S, D], BF16)
        for q in range(PAIRS):
            nc.sync.dma_start(out=x_all[:, 2 * q : 2 * q + 2, :], in_=c_att[:, 2 * q : 2 * q + 2, :])
        w2raw = const.tile([P, PACK, D], BF16)
        nc.sync.dma_start(out=w2raw[:], in_=mlp_kernel_2.rearrange("(j p) c -> p j c", p=P))
        gb2 = const.tile([P, 2, D], BF16)
        nc.sync.dma_start(out=gb2[:, 0, :], in_=mlp_gain_2.partition_broadcast(P))
        nc.sync.dma_start(out=gb2[:, 1, :], in_=mlp_bias_2.partition_broadcast(P))
        x_as_f32 = x_all[:].rearrange("p s d -> p (s d)").bitcast(F32)

        rows1f = const.tile([P, P], F32)
        nc.gpsimd.tensor_copy(out=rows1f[:], in_=rows1[:])
        gb1 = const.tile([P, 2 * PACK], F32)

        def gains1_to_partitions():
            gb1_ps = bank("yn", "gb1_ps")
            nc.tensor.transpose(out=gb1_ps[:, 0:P], in_=rows1f[:], identity=ident[:])
            nc.vector.tensor_copy(out=gb1[:], in_=gb1_ps[:, 0 : 2 * PACK])

        wg = {}
        wcodes = {}
        wscales = {}
        for label in ("w1", "w2"):
            wg[label] = const.tile([P, D, PACK], BF16, align_bytes=64, name=label + "_grouped")
            wcodes[label] = const.tile([P, D], U32, align_bytes=64, name=label + "_codes")
            wscales[label] = const.tile([P, D], U8, align_bytes=64, name=label + "_scales")
        xcodes = const.tile([P, S * P], U32, align_bytes=64)
        xscales = const.tile([P, S * P], U8, align_bytes=64)
        hcodes = const.tile([P, S * P], U32, align_bytes=64)
        hscales = const.tile([P, S * P], U8, align_bytes=64)

        def regroup_weight(label, raw, lo, hi):
            nc.vector.tensor_copy(
                out=wg[label][:, lo:hi, :].rearrange("p (c i) t -> p c t i", i=4),
                in_=raw[:, :, lo:hi].rearrange("p t (c i) -> p c t i", i=4),
            )

        def quantise_weight(label, lo, hi):
            nc.vector.quantize_mx(
                out=wcodes[label][:, lo:hi].bitcast(FP8X4),
                scales=wscales[label][:, lo:hi],
                in_=wg[label][:, lo:hi, :].rearrange("p c t -> p (c t)"),
            )

        def matmul_slot(dst, codes, scales, s, label):
            nc.tensor.matmul_mx(
                out=dst[:],
                lhsT=codes[:, s * P : (s + 1) * P].bitcast(FP8X4),
                lhsT_scale=scales[:, s * P : (s + 1) * P],
                rhs=wcodes[label][:].bitcast(FP8X4),
                rhs_scale=wscales[label][:],
                start=True,
                stop=True,
            )

        def x_transpose(q):
            if not is_pair(q):
                return
            xt = bank("zt", "xt")
            live["xt", q] = xt
            for i in range(2):
                for u in range(2):
                    col = (2 * q + i) * (D // 2) + u * P
                    nc.tensor.transpose(
                        out=xt[:, (2 * i + u) * P : (2 * i + u + 1) * P],
                        in_=x_as_f32[:, col : col + P],
                        identity=ident[:],
                    )

        def x_copy(q):
            if not is_pair(q):
                return
            xg = work.tile([P, 2 * D], BF16, align_bytes=64, tag="xg", bufs=4, name="xg")
            live["xg", q] = xg
            nc.scalar.copy(
                out=xg[:].bitcast(F32).rearrange("p (i k u) -> p i k u", i=2, u=2),
                in_=live["xt", q][:].rearrange("p (i u k) -> p i k u", i=2, u=2),
            )

        def x_quantise(q):
            if not is_pair(q):
                return
            cols = slice(2 * q * P, (2 * q + 2) * P)
            nc.vector.quantize_mx(out=xcodes[:, cols].bitcast(FP8X4), scales=xscales[:, cols], in_=live["xg", q][:])

        def moments(key, q, i, src):
            if i == 0:
                live[key + "st", q] = small.tile([P, 2, 6], F32, tag=key + "st", name=key + "st")
            nc.vector.bn_stats(out=live[key + "st", q][:, i, :], in_=live[src, q, i][:])

        def aggregate(key, q):
            live[key + "mv", q] = small.tile([P, 2, 2], F32, tag=key + "mv", name=key + "mv")
            for i in range(2):
                nc.vector.bn_aggr(out=live[key + "mv", q][:, i, :], in_=live[key + "st", q][:, i, :])

        def root(key, q, sums, divisor):
            sd = small.tile([P, 2], F32, tag=key + "sd", name=key + "sd")
            live[key + "sd", q] = sd
            nc.scalar.activation(out=sd[:], in_=sums, func=ACT.Sqrt, scale=1.0 / divisor)

        def add_eps(key, q):
            if not is_pair(q):
                return
            sde = small.tile([P, 2], F32, tag=key + "sde", name=key + "sde")
            live[key + "sde", q] = sde
            nc.vector.tensor_scalar_add(out=sde[:], in0=live[key + "sd", q][:], scalar1=EPS)

        def invert(key, q):
            if not is_pair(q):
                return
            r = small.tile([P, 2], F32, tag=key + "r", name=key + "r")
            live[key + "r", q] = r
            nc.vector.reciprocal(out=r[:], in_=live[key + "sde", q][:])

        def mm1_for_statistics(q, i):
            if is_pair(q):
                live["ys", q, i] = bank("ys", "ys")
                matmul_slot(live["ys", q, i], xcodes, xscales, 2 * q + i, "w1")

        def mm1_to_normalise(q, i):
            if is_pair(q):
                live["yn", q, i] = bank("yn", "yn")
                matmul_slot(live["yn", q, i], xcodes, xscales, 2 * q + i, "w1")

        def ln1_moments(q, i):
            if is_pair(q):
                moments("a", q, i, "ys")

        def ln1_aggregate(q):
            if is_pair(q):
                aggregate("a", q)

        def ln1_root(q):
            if is_pair(q):
                root("a", q, live["amv", q][:, :, 1], 1)

        def ln1_shift(q):
            if not is_pair(q):
                return
            nmr = small.tile([P, 2], F32, tag="anmr", name="anmr")
            live["anmr", q] = nmr
            nc.vector.scalar_tensor_tensor(
                out=nmr[:], in0=live["amv", q][:, :, 0], scalar=-1.0, in1=live["ar", q][:], op0=ALU.mult, op1=ALU.mult
            )

        def ln1_normalise(q, i):
            if not is_pair(q):
                return
            if i == 0:
                live["z", q] = work.tile([P, 2, D], F32, tag="z", name="z")
            nc.scalar.activation(
                out=live["z", q][:, i, :],
                in_=live["yn", q, i][:],
                func=ACT.Identity,
                bias=live["anmr", q][:, i : i + 1],
                scale=live["ar", q][:, i : i + 1],
            )

        def z_transpose(q):
            if not is_pair(q):
                return
            zts = [bank("zt", "zt"), bank("zt", "zt")]
            live["zt", q] = zts
            for i in range(2):
                for j in range(PACK):
                    col = (2 * (j % 2) + i) * P
                    nc.tensor.transpose(
                        out=zts[j // 2][:, col : col + P],
                        in_=live["z", q][:, i, j * P : (j + 1) * P],
                        identity=ident[:],
                    )

        def h_activate(q):
            if not is_pair(q):
                return
            live["hp", q] = work.tile([P, PACK, 2 * P], BF16, tag="hp", name="hp")
            for j in range(PACK):
                nc.scalar.activation(
                    out=live["hp", q][:, j, :],
                    in_=live["zt", q][j // 2][:, (j % 2) * 2 * P : (j % 2 + 1) * 2 * P],
                    func=ACT.Relu,
                    bias=gb1[:, PACK + j : PACK + j + 1],
                    scale=gb1[:, j : j + 1],
                )

        def h_regroup(q):
            if not is_pair(q):
                return
            hg = work.tile([P, 2 * P, PACK], BF16, align_bytes=64, tag="hg", name="hg")
            live["hg", q] = hg
            nc.vector.tensor_copy(
                out=hg[:].rearrange("p (c i) t -> p c t i", i=4),
                in_=live["hp", q][:].rearrange("p t (c i) -> p c t i", i=4),
            )

        def h_quantise(q):
            if not is_pair(q):
                return
            cols = slice(2 * q * P, (2 * q + 2) * P)
            nc.vector.quantize_mx(
                out=hcodes[:, cols].bitcast(FP8X4),
                scales=hscales[:, cols],
                in_=live["hg", q][:].rearrange("p k t -> p (k t)"),
            )

        def mm2(q):
            if not is_pair(q):
                return
            for i in range(2):
                live["y2", q, i] = bank(BANKS_OF_Y2[q], "y2")
                matmul_slot(live["y2", q, i], hcodes, hscales, 2 * q + i, "w2")

        def ln2_copy_and_sum(q, i):
            if not on_scalar(q):
                return
            if i == 0:
                live["y2s", q] = work.tile([P, 2, D], F32, tag="y2s", name="y2s")
                live["tot", q] = small.tile([P, 2], F32, tag="tot", name="tot")
            nc.scalar.activation(
                out=live["y2s", q][:, i, :],
                in_=live["y2", q, i][:],
                func=ACT.Identity,
                accum_out=live["tot", q][:, i : i + 1],
            )

        def ln2_minus_mean(q):
            if not on_scalar(q):
                return
            negmu = small.tile([P, 2], F32, tag="negmu", name="negmu")
            live["negmu", q] = negmu
            nc.scalar.mul(out=negmu[:], in_=live["tot", q][:], mul=-1.0 / D)

        def ln2_squared_deviations(q):
            if not on_scalar(q):
                return
            ssq = small.tile([P, 2], F32, tag="ssq", name="ssq")
            live["ssq", q] = ssq
            for i in range(2):
                junk = work.tile([P, D], BF16, tag="junk", bufs=2, name="junk")
                nc.scalar.activation(
                    out=junk[:],
                    in_=live["y2s", q][:, i, :],
                    func=ACT.Square,
                    bias=live["negmu", q][:, i : i + 1],
                    accum_out=ssq[:, i : i + 1],
                )

        def ln2_moments(q, i):
            if is_pair(q):
                moments("b", q, i, "y2")

        def ln2_aggregate(q):
            if is_pair(q):
                aggregate("b", q)

        def ln2_root(q):
            if on_vector(q):
                root("b", q, live["bmv", q][:, :, 1], 1)
            elif on_scalar(q):
                root("b", q, live["ssq", q][:], D)

        def ln2_centre_and_gain(q, i):
            if not is_pair(q):
                return
            if i == 0:
                live["t", q] = work.tile([P, 2, D], F32, tag="t", name="t")
            if on_vector(q):
                nc.vector.scalar_tensor_tensor(
                    out=live["t", q][:, i, :],
                    in0=live["y2", q, i][:],
                    scalar=live["bmv", q][:, i, 0:1],
                    in1=gb2[:, 0, :],
                    op0=ALU.subtract,
                    op1=ALU.mult,
                )
            else:
                nc.vector.scalar_tensor_tensor(
                    out=live["t", q][:, i, :],
                    in0=live["y2s", q][:, i, :],
                    scalar=live["negmu", q][:, i : i + 1],
                    in1=gb2[:, 0, :],
                    op0=ALU.add,
                    op1=ALU.mult,
                )

        def ln2_scale_bias_store(q, i):
            if not is_pair(q):
                return
            if i == 0:
                live["o", q] = work.tile([P, 2, D], F32, tag="o", bufs=4, name="o")
            o = live["o", q]
            nc.vector.scalar_tensor_tensor(
                out=o[:, i, :],
                in0=live["t", q][:, i, :],
                scalar=live["br", q][:, i : i + 1],
                in1=gb2[:, 1, :],
                op0=ALU.mult,
                op1=ALU.add,
            )
            if q >= PAIRS - 2:
                nc.sync.dma_start(out=out[:, 2 * q + i, :], in_=o[:, i, :])
            elif i == 1:
                nc.sync.dma_start(out=out[:, 2 * q : 2 * q + 2, :], in_=o[:])

        regroup_weight("w1", w1raw, 0, 256)
        regroup_weight("w1", w1raw, 256, 512)
        quantise_weight("w1", 0, 256)
        quantise_weight("w1", 256, 512)

        for n in range(-7, PAIRS + 4):
            starting = vector_pair_started_in(n)
            started = vector_pair_started_in(n - 1)
            x_transpose(n + 7)
            if n == -1:
                gains1_to_partitions()
            ln1_normalise(n, 0)
            ln1_normalise(n, 1)
            ln1_moments(n + 2, 0)
            ln2_moments(starting, 0)
            ln2_centre_and_gain(started, 0)
            mm1_for_statistics(n + 3, 0)
            mm1_to_normalise(n + 1, 0)
            mm1_to_normalise(n + 1, 1)
            add_eps("a", n + 1)
            add_eps("b", started)
            ln1_moments(n + 2, 1)
            ln2_moments(starting, 1)
            ln2_centre_and_gain(started, 1)
            mm1_for_statistics(n + 3, 1)
            mm2(vector_pair_started_in(n + 1))
            z_transpose(n)
            invert("a", n + 1)
            invert("b", started)
            x_copy(n + 7)
            h_regroup(n - 2)
            ln1_aggregate(n + 2)
            ln2_aggregate(starting)
            ln1_shift(n + 1)
            h_quantise(n - 3)
            x_quantise(n + 4)
            ln2_scale_bias_store(vector_pair_started_in(n - 3), 0)
            ln2_scale_bias_store(vector_pair_started_in(n - 3), 1)
            if -1 <= n < 3:
                regroup_weight("w2", w2raw, 128 * (n + 1), 128 * (n + 2))
            if 3 <= n < 5:
                quantise_weight("w2", 256 * (n - 3), 256 * (n - 2))
            h_activate(n - 1)
            ln1_root(n + 2)
            ln2_root(starting)

        first = len(VECTOR_PAIRS)
        mm2(first)
        mm2(first + 1)
        for k in range(first, PAIRS + 2):
            mm2(k + 2)
            ln2_copy_and_sum(k, 0)
            ln2_minus_mean(k - 1)
            ln2_root(scalar_pair(k - 2))
            ln2_copy_and_sum(k, 1)
            ln2_squared_deviations(k - 1)
            add_eps("b", scalar_pair(k - 2))
            ln2_centre_and_gain(scalar_pair(k - 1), 0)
            invert("b", scalar_pair(k - 2))
            ln2_centre_and_gain(scalar_pair(k - 1), 1)
            ln2_scale_bias_store(scalar_pair(k - 2), 0)
            ln2_scale_bias_store(scalar_pair(k - 2), 1)
